import numpy as np
import ml_dtypes


def mxq(x, axis, fmt="e4m3"):
    dtype, down = {"e4m3": (ml_dtypes.float8_e4m3fn, 7), "e5m2": (ml_dtypes.float8_e5m2, 14)}[fmt]
    v = np.moveaxis(np.asarray(x, np.float32).astype(ml_dtypes.bfloat16).astype(np.float64), axis, -1)
    blocks = v.reshape(v.shape[:-1] + (-1, 32))
    amax = np.abs(blocks).max(-1, keepdims=True)
    byte = np.maximum(np.where(amax > 0, np.frexp(amax)[1] - 1 + 127, 0) - down, 1)
    scale = np.exp2(byte - 127.0)
    codes = (blocks / scale).astype(np.float32).astype(dtype).astype(np.float64)
    return np.moveaxis((codes * scale).reshape(v.shape), -1, axis)


WIDE = False


def mx_kscale(k):
    if not WIDE:
        return np.ones(k)
    levels = np.array([20, -20, 10, -10, 0])
    a = np.random.permutation(np.resize(levels, k // 512 * 4)).reshape(k // 512, 4)
    idx = np.arange(k)
    return np.exp2(a[idx // 512, idx % 128 // 32])


BF16 = ml_dtypes.bfloat16


def bf(x):
    return np.asarray(x, np.float32).astype(BF16)


def f64(x):
    return np.asarray(x).astype(np.float64)


B, E, N = 4096, 512, 1024
CLIP_TANH = 10.0
DENS = 0.25


def setup_inputs():
    u = mx_kscale(E)
    x = bf(np.random.standard_normal((B, E)))
    llr = bf(np.random.standard_normal((B, N)))
    ow0 = bf(np.random.standard_normal((E, E)) * 1.4 / np.sqrt(DENS * E))
    lw = bf(np.random.standard_normal((N, E)) * 1.4 / np.sqrt(DENS * N))
    m_odd = bf((np.random.random((E, E)) < DENS).astype(np.float64))
    m_skip = bf((np.random.random((N, E)) < DENS).astype(np.float64))
    g = bf(np.random.standard_normal((B, E)) * np.exp2(np.random.randint(-12, 1, (B, 1))) * 16.0 * u)
    z = f64(x) @ (f64(m_odd) * f64(ow0)) + f64(llr) @ (f64(m_skip) * f64(lw))
    return {"x": x,
            "llr": llr,
            "odd_weights": bf(f64(ow0) / u[None, :]),
            "llr_weights": lw,
            "w_odd2even_mask": m_odd,
            "w_skipconn2even_mask": m_skip,
            "z": np.asarray(z, np.float32),
            "grad_out": g}


def reference(x, llr, odd_weights, llr_weights, w_odd2even_mask, w_skipconn2even_mask, z, grad_out):
    zf = f64(z)
    t = np.tanh(0.5 * zf)
    inside = (np.abs(zf) <= CLIP_TANH).astype(np.float64)
    dz = f64(grad_out) * (0.5 * (1.0 - t * t) * inside)
    wm = f64(w_odd2even_mask) * f64(odd_weights)
    return mxq(dz, 1, "e5m2") @ mxq(wm, 1, "e4m3").T

@@ -1,0 +1,222 @@
+from contextlib import ExitStack
+
+import concourse.mybir as mybir
+from concourse.masks import make_identity
+
+F32 = mybir.dt.float32
+BF16 = mybir.dt.bfloat16
+I32 = mybir.dt.int32
+U32 = mybir.dt.uint32
+U8 = mybir.dt.uint8
+E4M3X4 = mybir.dt.float8_e4m3fn_x4
+E5M2X4 = mybir.dt.float8_e5m2_x4
+ALU = mybir.AluOpType
+ACT = mybir.ActivationFunctionType
+
+P = 128
+PACK = 4
+TOKENS = 4096
+FEATURES = 512
+CLIP = 10.0
+BLOCKS = TOKENS // P
+PAIRS = BLOCKS // 2
+ROW_BLOCKS = FEATURES // P
+
+FLOPS = 2 * TOKENS * FEATURES * FEATURES
+BYTES = TOKENS * FEATURES * (4 + 2 + 4) + 2 * FEATURES * FEATURES * 2
+
+
+def tile_oddlayer_t_v_kernel(
+    tc, x, llr, odd_weights, llr_weights, w_odd2even_mask, w_skipconn2even_mask, z, grad_out, out
+):
+    nc = tc.nc
+    with ExitStack() as stack:
+        stack.enter_context(tc.manual_schedule())
+        consts = stack.enter_context(tc.tile_pool(name="consts", bufs=1))
+        z_pool = stack.enter_context(tc.tile_pool(name="z_pool", bufs=PAIRS))
+        g_pool = stack.enter_context(tc.tile_pool(name="g_pool", bufs=PAIRS))
+        work = stack.enter_context(tc.tile_pool(name="work", bufs=4))
+        out_pool = stack.enter_context(tc.tile_pool(name="out_pool", bufs=10))
+        psum_a = stack.enter_context(tc.psum_pool(name="psum_a", bufs=4))
+        psum_g = stack.enter_context(tc.psum_pool(name="psum_g", bufs=2))
+        psum_o = stack.enter_context(tc.psum_pool(name="psum_o", bufs=2))
+
+        z_view = z.rearrange("(q p h) k -> q p h k", p=P, h=2)
+        g_view = grad_out.rearrange("(q p h) k -> q p h k", p=P, h=2)
+        out_view = out.rearrange("(q p h) i -> q p h i", p=P, h=2)
+
+        z_tiles = []
+        g_tiles = []
+        w_sb = consts.tile([P, ROW_BLOCKS, FEATURES], BF16)
+        m_sb = consts.tile([P, ROW_BLOCKS, FEATURES], BF16)
+        for q in range(PAIRS):
+            z_sb = z_pool.tile([P, 2, FEATURES], F32)
+            nc.sync.dma_start(out=z_sb[:], in_=z_view[q])
+            z_tiles.append(z_sb)
+            if q == 0:
+                nc.sync.dma_start(out=w_sb[:], in_=odd_weights.rearrange("(r p) k -> p r k", p=P))
+                nc.sync.dma_start(out=m_sb[:], in_=w_odd2even_mask.rearrange("(r p) k -> p r k", p=P))
+            g_sb = g_pool.tile([P, 2, FEATURES], BF16)
+            nc.sync.dma_start(out=g_sb[:], in_=g_view[q])
+            g_tiles.append(g_sb)
+
+        ident_f32 = consts.tile([P, P], F32)
+        make_identity(nc, ident_f32[:])
+        ident_bf16 = consts.tile([P, P], BF16)
+        make_identity(nc, ident_bf16[:])
+
+        wm_sb = consts.tile([P, ROW_BLOCKS, FEATURES], BF16)
+        wm_grouped = consts.tile([P, FEATURES, PACK], BF16, align_bytes=64)
+        wm_codes = consts.tile([P, FEATURES], U32, align_bytes=64)
+        wm_scales = consts.tile([P, FEATURES], U8, align_bytes=64)
+        wmT_tiles = {}
+        a_tiles = {}
+        aT_tiles = {}
+        gT_tiles = {}
+        th_tiles = {}
+        sq_tiles = {}
+        slope_tiles = {}
+        dz2_tiles = {}
+        code_tiles = {}
+        out_ps_tiles = {}
+        out_sb_tiles = {}
+
+        def is_block(n):
+            return 0 <= n < BLOCKS
+
+        def is_row_block(r):
+            return 0 <= r < ROW_BLOCKS
+
+        def transpose_weights():
+            nc.vector.tensor_tensor(out=wm_sb[:], in0=w_sb[:], in1=m_sb[:], op=ALU.mult)
+            for half in range(ROW_BLOCKS // 2):
+                wmT_ps = psum_o.tile([P, 2, PACK, P], BF16, tag="out_ps")
+                for h in range(2):
+                    for j in range(PACK):
+                        nc.tensor.transpose(
+                            wmT_ps[:, h, j, :], wm_sb[:, 2 * half + h, j * P : (j + 1) * P], ident_bf16[:]
+                        )
+                wmT_tiles[half] = wmT_ps
+
+        def group_weights(r):
+            nc.vector.tensor_copy(
+                out=wm_grouped[:, r * P : (r + 1) * P, :],
+                in_=wmT_tiles[r // 2][:, r % 2].rearrange("p j i -> p i j"),
+            )
+
+        def quantise_weights():
+            nc.vector.quantize_mx(
+                out=wm_codes[:].bitcast(E4M3X4),
+                scales=wm_scales[:],
+                in_=wm_grouped[:].rearrange("p i j -> p (i j)"),
+            )
+
+        def absolute(q):
+            a_sb = work.tile([P, 2, FEATURES], F32)
+            nc.vector.tensor_single_scalar(
+                out=a_sb[:].bitcast(I32), in_=z_tiles[q][:].bitcast(I32), scalar=0x7FFFFFFF, op=ALU.bitwise_and
+            )
+            a_tiles[q] = a_sb
+
+        def transpose_a(n):
+            aT_ps = psum_a.tile([P, PACK, P], F32)
+            for j in range(PACK):
+                nc.tensor.transpose(aT_ps[:, j, :], a_tiles[n // 2][:, n % 2, j * P : (j + 1) * P], ident_f32[:])
+            aT_tiles[n] = aT_ps
+
+        def transpose_g(q):
+            gT_ps = psum_g.tile([P, 2, PACK, P], BF16)
+            for h in range(2):
+                for j in range(PACK):
+                    nc.tensor.transpose(gT_ps[:, h, j, :], g_tiles[q][:, h, j * P : (j + 1) * P], ident_bf16[:])
+            gT_tiles[q] = gT_ps
+
+        def tanh(n):
+            th = work.tile([P, P, PACK], F32)
+            nc.scalar.activation(
+                out=th[:], in_=aT_tiles[n][:].rearrange("p j n -> p n j"), func=ACT.Tanh, scale=0.5
+            )
+            th_tiles[n] = th
+
+        def square(n):
+            sq = work.tile([P, P, PACK], F32)
+            nc.scalar.activation(out=sq[:], in_=th_tiles[n][:], func=ACT.Square)
+            sq_tiles[n] = sq
+
+        def slope_of(n):
+            slope = work.tile([P, P, PACK], F32)
+            nc.vector.scalar_tensor_tensor(
+                out=slope[:], in0=aT_tiles[n][:].rearrange("p j n -> p n j"), scalar=CLIP,
+                in1=sq_tiles[n][:], op0=ALU.is_le, op1=ALU.subtract,
+            )
+            slope_tiles[n] = slope
+
+        def times_g(n):
+            if n % 2 == 0:
+                dz2 = work.tile([P, 2, P, PACK], BF16, align_bytes=64)
+                dz2_tiles[n // 2] = dz2
+            nc.vector.scalar_tensor_tensor(
+                out=dz2_tiles[n // 2][:, n % 2], in0=slope_tiles[n][:], scalar=0.0,
+                in1=gT_tiles[n // 2][:, n % 2].rearrange("p j n -> p n j"), op0=ALU.max, op1=ALU.mult,
+            )
+
+        def quantise(q):
+            dz_codes = work.tile([P, 2 * P], U32, align_bytes=64)
+            dz_scales = work.tile([P, 2 * P], U8, align_bytes=64)
+            nc.vector.quantize_mx(
+                out=dz_codes[:].bitcast(E5M2X4),
+                scales=dz_scales[:],
+                in_=dz2_tiles[q][:].rearrange("p h n j -> p (h n j)"),
+            )
+            code_tiles[q] = (dz_codes, dz_scales)
+
+        def multiply(n):
+            dz_codes, dz_scales = code_tiles[n // 2]
+            cols = slice((n % 2) * P, (n % 2 + 1) * P)
+            out_ps = psum_o.tile([P, FEATURES], F32)
+            nc.tensor.matmul_mx(
+                out=out_ps[:],
+                lhsT=dz_codes[:, cols].bitcast(E5M2X4),
+                lhsT_scale=dz_scales[:, cols],
+                rhs=wm_codes[:].bitcast(E4M3X4),
+                rhs_scale=wm_scales[:],
+                start=True,
+                stop=True,
+            )
+            out_ps_tiles[n] = out_ps
+
+        def leave_psum(n):
+            if n % 2 == 0:
+                out_sb = out_pool.tile([P, 2, FEATURES], F32)
+                out_sb_tiles[n // 2] = out_sb
+            nc.scalar.mul(out=out_sb_tiles[n // 2][:, n % 2, :], in_=out_ps_tiles[n][:], mul=0.5)
+            if n % 2 == 1:
+                nc.sync.dma_start(out=out_view[n // 2], in_=out_sb_tiles[n // 2][:])
+
+        for s in range(-4, BLOCKS + 6):
+            if is_block(s - 4):
+                multiply(s - 4)
+            if is_block(s + 3):
+                transpose_a(s + 3)
+            if s % 2 == 1 and is_block(s + 1):
+                transpose_g((s + 1) // 2)
+            if is_block(s + 2):
+                tanh(s + 2)
+            if is_block(s - 5):
+                leave_psum(s - 5)
+            if is_block(s + 2):
+                square(s + 2)
+            if is_block(s):
+                slope_of(s)
+            if s % 2 == 0 and is_block(s + 4):
+                absolute((s + 4) // 2)
+            if s % 2 == 1 and is_block(s - 3):
+                quantise((s - 3) // 2)
+            if s == -3:
+                transpose_weights()
+            if is_row_block(s + 1):
+                group_weights(s + 1)
+            if s + 1 == ROW_BLOCKS:
+                quantise_weights()
+            if is_block(s - 1):
+                times_g(s - 1)

@@ -174,15 +174,16 @@ def tile_oddlayer_t_v_kernel(
             dz_codes, dz_scales = code_tiles[n // 2]
             cols = slice((n % 2) * P, (n % 2 + 1) * P)
             out_ps = psum_o.tile([P, FEATURES], F32)
-            nc.tensor.matmul_mx(
-                out=out_ps[:],
-                lhsT=dz_codes[:, cols].bitcast(E5M2X4),
-                lhsT_scale=dz_scales[:, cols],
-                rhs=wm_codes[:].bitcast(E4M3X4),
-                rhs_scale=wm_scales[:],
-                start=True,
-                stop=True,
-            )
+            for repeat in range(2):
+                nc.tensor.matmul_mx(
+                    out=out_ps[:],
+                    lhsT=dz_codes[:, cols].bitcast(E5M2X4),
+                    lhsT_scale=dz_scales[:, cols],
+                    rhs=wm_codes[:].bitcast(E4M3X4),
+                    rhs_scale=wm_scales[:],
+                    start=True,
+                    stop=True,
+                )
             out_ps_tiles[n] = out_ps
 
         def leave_psum(n):

@@ -87,8 +87,10 @@ def tile_oddlayer_t_v_kernel(
         def is_row_block(r):
             return 0 <= r < ROW_BLOCKS
 
-        def transpose_weights():
+        def mask_weights():
             nc.vector.tensor_tensor(out=wm_sb[:], in0=w_sb[:], in1=m_sb[:], op=ALU.mult)
+
+        def transpose_weights():
             for half in range(ROW_BLOCKS // 2):
                 wmT_ps = psum_o.tile([P, 2, PACK, P], BF16, tag="out_ps")
                 for h in range(2):
@@ -174,16 +176,15 @@ def tile_oddlayer_t_v_kernel(
             dz_codes, dz_scales = code_tiles[n // 2]
             cols = slice((n % 2) * P, (n % 2 + 1) * P)
             out_ps = psum_o.tile([P, FEATURES], F32)
-            for repeat in range(2):
-                nc.tensor.matmul_mx(
-                    out=out_ps[:],
-                    lhsT=dz_codes[:, cols].bitcast(E5M2X4),
-                    lhsT_scale=dz_scales[:, cols],
-                    rhs=wm_codes[:].bitcast(E4M3X4),
-                    rhs_scale=wm_scales[:],
-                    start=True,
-                    stop=True,
-                )
+            nc.tensor.matmul_mx(
+                out=out_ps[:],
+                lhsT=dz_codes[:, cols].bitcast(E5M2X4),
+                lhsT_scale=dz_scales[:, cols],
+                rhs=wm_codes[:].bitcast(E4M3X4),
+                rhs_scale=wm_scales[:],
+                start=True,
+                stop=True,
+            )
             out_ps_tiles[n] = out_ps
 
         def leave_psum(n):
@@ -195,18 +196,6 @@ def tile_oddlayer_t_v_kernel(
                 nc.sync.dma_start(out=out_view[n // 2], in_=out_sb_tiles[n // 2][:])
 
         for s in range(-4, BLOCKS + 6):
-            if is_block(s - 4):
-                multiply(s - 4)
-            if is_block(s + 3):
-                transpose_a(s + 3)
-            if s % 2 == 1 and is_block(s + 1):
-                transpose_g((s + 1) // 2)
-            if is_block(s + 2):
-                tanh(s + 2)
-            if is_block(s - 5):
-                leave_psum(s - 5)
-            if is_block(s + 2):
-                square(s + 2)
             if is_block(s):
                 slope_of(s)
             if s % 2 == 0 and is_block(s + 4):
@@ -214,10 +203,28 @@ def tile_oddlayer_t_v_kernel(
             if s % 2 == 1 and is_block(s - 3):
                 quantise((s - 3) // 2)
             if s == -3:
-                transpose_weights()
+                mask_weights()
             if is_row_block(s + 1):
                 group_weights(s + 1)
             if s + 1 == ROW_BLOCKS:
                 quantise_weights()
             if is_block(s - 1):
                 times_g(s - 1)
+            if is_block(s + 2):
+                tanh(s + 2)
+            if is_block(s - 5):
+                leave_psum(s - 5)
+            if is_block(s + 2):
+                square(s + 2)
+            if s == -3:
+                transpose_weights()
+            if s % 2 == 0:
+                if is_block(s + 3):
+                    transpose_a(s + 3)
+                if is_block(s + 4):
+                    transpose_a(s + 4)
+                if is_block(s - 4):
+                    multiply(s - 4)
+                    multiply(s - 3)
+                if is_block(s + 2):
+                    transpose_g((s + 2) // 2)

@@ -87,6 +87,9 @@ def tile_oddlayer_t_v_kernel(
         def is_row_block(r):
             return 0 <= r < ROW_BLOCKS
 
+        def through_vector(n):
+            return n % 8 == 7
+
         def mask_weights():
             nc.vector.tensor_tensor(out=wm_sb[:], in0=w_sb[:], in1=m_sb[:], op=ALU.mult)
 
@@ -101,7 +104,7 @@ def tile_oddlayer_t_v_kernel(
                 wmT_tiles[half] = wmT_ps
 
         def group_weights(r):
-            nc.vector.tensor_copy(
+            nc.scalar.copy(
                 out=wm_grouped[:, r * P : (r + 1) * P, :],
                 in_=wmT_tiles[r // 2][:, r % 2].rearrange("p j i -> p i j"),
             )
@@ -127,10 +130,12 @@ def tile_oddlayer_t_v_kernel(
             aT_tiles[n] = aT_ps
 
         def transpose_g(q):
-            gT_ps = psum_g.tile([P, 2, PACK, P], BF16)
+            gT_ps = psum_g.tile([P, PACK, 2 * P], BF16)
             for h in range(2):
                 for j in range(PACK):
-                    nc.tensor.transpose(gT_ps[:, h, j, :], g_tiles[q][:, h, j * P : (j + 1) * P], ident_bf16[:])
+                    nc.tensor.transpose(
+                        gT_ps[:, j, h * P : (h + 1) * P], g_tiles[q][:, h, j * P : (j + 1) * P], ident_bf16[:]
+                    )
             gT_tiles[q] = gT_ps
 
         def tanh(n):
@@ -146,21 +151,21 @@ def tile_oddlayer_t_v_kernel(
             sq_tiles[n] = sq
 
         def slope_of(n):
-            slope = work.tile([P, P, PACK], F32)
+            if n % 2 == 0:
+                slope = work.tile([P, 2, P, PACK], F32)
+                slope_tiles[n // 2] = slope
             nc.vector.scalar_tensor_tensor(
-                out=slope[:], in0=aT_tiles[n][:].rearrange("p j n -> p n j"), scalar=CLIP,
+                out=slope_tiles[n // 2][:, n % 2], in0=aT_tiles[n][:].rearrange("p j n -> p n j"), scalar=CLIP,
                 in1=sq_tiles[n][:], op0=ALU.is_le, op1=ALU.subtract,
             )
-            slope_tiles[n] = slope
 
-        def times_g(n):
-            if n % 2 == 0:
-                dz2 = work.tile([P, 2, P, PACK], BF16, align_bytes=64)
-                dz2_tiles[n // 2] = dz2
+        def times_g(q):
+            dz2 = work.tile([P, 2 * P, PACK], BF16, align_bytes=64)
             nc.vector.scalar_tensor_tensor(
-                out=dz2_tiles[n // 2][:, n % 2], in0=slope_tiles[n][:], scalar=0.0,
-                in1=gT_tiles[n // 2][:, n % 2].rearrange("p j n -> p n j"), op0=ALU.max, op1=ALU.mult,
+                out=dz2[:], in0=slope_tiles[q][:].rearrange("p h n j -> p (h n) j"), scalar=0.0,
+                in1=gT_tiles[q][:].rearrange("p j m -> p m j"), op0=ALU.max, op1=ALU.mult,
             )
+            dz2_tiles[q] = dz2
 
         def quantise(q):
             dz_codes = work.tile([P, 2 * P], U32, align_bytes=64)
@@ -168,7 +173,7 @@ def tile_oddlayer_t_v_kernel(
             nc.vector.quantize_mx(
                 out=dz_codes[:].bitcast(E5M2X4),
                 scales=dz_scales[:],
-                in_=dz2_tiles[q][:].rearrange("p h n j -> p (h n j)"),
+                in_=dz2_tiles[q][:].rearrange("p m j -> p (m j)"),
             )
             code_tiles[q] = (dz_codes, dz_scales)
 
@@ -191,7 +196,10 @@ def tile_oddlayer_t_v_kernel(
             if n % 2 == 0:
                 out_sb = out_pool.tile([P, 2, FEATURES], F32)
                 out_sb_tiles[n // 2] = out_sb
-            nc.scalar.mul(out=out_sb_tiles[n // 2][:, n % 2, :], in_=out_ps_tiles[n][:], mul=0.5)
+            if through_vector(n):
+                nc.vector.tensor_scalar_mul(out=out_sb_tiles[n // 2][:, n % 2, :], in0=out_ps_tiles[n][:], scalar1=0.5)
+            else:
+                nc.scalar.mul(out=out_sb_tiles[n // 2][:, n % 2, :], in_=out_ps_tiles[n][:], mul=0.5)
             if n % 2 == 1:
                 nc.sync.dma_start(out=out_view[n // 2], in_=out_sb_tiles[n // 2][:])
 
@@ -204,15 +212,17 @@ def tile_oddlayer_t_v_kernel(
                 quantise((s - 3) // 2)
             if s == -3:
                 mask_weights()
-            if is_row_block(s + 1):
-                group_weights(s + 1)
-            if s + 1 == ROW_BLOCKS:
+            if s == ROW_BLOCKS:
                 quantise_weights()
-            if is_block(s - 1):
-                times_g(s - 1)
+            if is_block(s - 5) and through_vector(s - 5):
+                leave_psum(s - 5)
+            if s % 2 == 0 and is_block(s - 2):
+                times_g((s - 2) // 2)
             if is_block(s + 2):
                 tanh(s + 2)
-            if is_block(s - 5):
+            if is_row_block(s):
+                group_weights(s)
+            if is_block(s - 5) and not through_vector(s - 5):
                 leave_psum(s - 5)
             if is_block(s + 2):
                 square(s + 2)

@@ -45,25 +45,54 @@ def tile_oddlayer_t_v_kernel(
         g_view = grad_out.rearrange("(q p h) k -> q p h k", p=P, h=2)
         out_view = out.rearrange("(q p h) i -> q p h i", p=P, h=2)
 
+        w_view = odd_weights.rearrange("(r p) k -> p r k", p=P)
+        m_view = w_odd2even_mask.rearrange("(r p) k -> p r k", p=P)
         z_tiles = []
         g_tiles = []
         w_sb = consts.tile([P, ROW_BLOCKS, FEATURES], BF16)
         m_sb = consts.tile([P, ROW_BLOCKS, FEATURES], BF16)
-        for q in range(PAIRS):
+
+        def load_z(q):
             z_sb = z_pool.tile([P, 2, FEATURES], F32)
-            nc.sync.dma_start(out=z_sb[:], in_=z_view[q])
-            z_tiles.append(z_sb)
             if q == 0:
-                nc.sync.dma_start(out=w_sb[:], in_=odd_weights.rearrange("(r p) k -> p r k", p=P))
-                nc.sync.dma_start(out=m_sb[:], in_=w_odd2even_mask.rearrange("(r p) k -> p r k", p=P))
+                for h in range(2):
+                    nc.sync.dma_start(out=z_sb[:, h, :], in_=z_view[q][:, h, :])
+            else:
+                nc.sync.dma_start(out=z_sb[:], in_=z_view[q])
+            z_tiles.append(z_sb)
+
+        def load_g(q):
             g_sb = g_pool.tile([P, 2, FEATURES], BF16)
             nc.sync.dma_start(out=g_sb[:], in_=g_view[q])
             g_tiles.append(g_sb)
+
+        load_z(0)
+        for h in range(2):
+            rows = slice(2 * h, 2 * h + 2)
+            nc.sync.dma_start(out=w_sb[:, rows, :], in_=w_view[:, rows, :])
+            nc.sync.dma_start(out=m_sb[:, rows, :], in_=m_view[:, rows, :])
+            if h == 0:
+                load_z(1)
+        load_g(0)
+        for q in range(2, PAIRS):
+            load_z(q)
+            load_g(q - 1)
+        load_g(PAIRS - 1)
 
         ident_f32 = consts.tile([P, P], F32)
         make_identity(nc, ident_f32[:])
         ident_bf16 = consts.tile([P, P], BF16)
         make_identity(nc, ident_bf16[:])
+
+        warm = consts.tile([P, FEATURES], BF16)
+        nc.vector.memset(warm[:], 0.0)
+
+        def keep_warm(passes):
+            for i in range(passes):
+                junk = psum_o.tile([P, FEATURES], F32, tag="out_ps")
+                nc.tensor.matmul(out=junk[:], lhsT=warm[:, :P], rhs=warm[:], start=True, stop=True)
+
+        keep_warm(3)
 
         wm_sb = consts.tile([P, ROW_BLOCKS, FEATURES], BF16)
         wm_grouped = consts.tile([P, FEATURES, PACK], BF16, align_bytes=64)
@@ -88,20 +117,18 @@ def tile_oddlayer_t_v_kernel(
             return 0 <= r < ROW_BLOCKS
 
         def through_vector(n):
-            return n % 8 == 7
+            return n % 8 == 7 and n < BLOCKS - 4
 
-        def mask_weights():
-            nc.vector.tensor_tensor(out=wm_sb[:], in0=w_sb[:], in1=m_sb[:], op=ALU.mult)
+        def mask_weights(half):
+            rows = slice(2 * half, 2 * half + 2)
+            nc.vector.tensor_tensor(out=wm_sb[:, rows, :], in0=w_sb[:, rows, :], in1=m_sb[:, rows, :], op=ALU.mult)
 
-        def transpose_weights():
-            for half in range(ROW_BLOCKS // 2):
+        def transpose_weights(r):
+            if r % 2 == 0:
                 wmT_ps = psum_o.tile([P, 2, PACK, P], BF16, tag="out_ps")
-                for h in range(2):
-                    for j in range(PACK):
-                        nc.tensor.transpose(
-                            wmT_ps[:, h, j, :], wm_sb[:, 2 * half + h, j * P : (j + 1) * P], ident_bf16[:]
-                        )
-                wmT_tiles[half] = wmT_ps
+                wmT_tiles[r // 2] = wmT_ps
+            for j in range(PACK):
+                turn_bf16(wmT_tiles[r // 2][:, r % 2, j, :], wm_sb[:, r, j * P : (j + 1) * P], True)
 
         def group_weights(r):
             nc.scalar.copy(
@@ -116,12 +143,13 @@ def tile_oddlayer_t_v_kernel(
                 in_=wm_grouped[:].rearrange("p i j -> p (i j)"),
             )
 
-        def absolute(q):
-            a_sb = work.tile([P, 2, FEATURES], F32)
+        def absolute(q, h):
+            if q not in a_tiles:
+                a_sb = work.tile([P, 2, FEATURES], F32)
+                a_tiles[q] = a_sb
             nc.vector.tensor_single_scalar(
-                out=a_sb[:].bitcast(I32), in_=z_tiles[q][:].bitcast(I32), scalar=0x7FFFFFFF, op=ALU.bitwise_and
+                out=a_tiles[q][:, h, :].bitcast(I32), in_=z_tiles[q][:, h, :].bitcast(I32), scalar=0x7FFFFFFF, op=ALU.bitwise_and
             )
-            a_tiles[q] = a_sb
 
         def transpose_a(n):
             aT_ps = psum_a.tile([P, PACK, P], F32)
@@ -129,14 +157,19 @@ def tile_oddlayer_t_v_kernel(
                 nc.tensor.transpose(aT_ps[:, j, :], a_tiles[n // 2][:, n % 2, j * P : (j + 1) * P], ident_f32[:])
             aT_tiles[n] = aT_ps
 
-        def transpose_g(q):
-            gT_ps = psum_g.tile([P, PACK, 2 * P], BF16)
-            for h in range(2):
-                for j in range(PACK):
-                    nc.tensor.transpose(
-                        gT_ps[:, j, h * P : (h + 1) * P], g_tiles[q][:, h, j * P : (j + 1) * P], ident_bf16[:]
-                    )
-            gT_tiles[q] = gT_ps
+        def turn_bf16(out_ps, in_sb, as_matmul):
+            if as_matmul:
+                nc.tensor.matmul(out=out_ps, lhsT=in_sb, rhs=ident_bf16[:], start=True, stop=True)
+            else:
+                nc.tensor.transpose(out_ps, in_sb, ident_bf16[:])
+
+        def transpose_g(n):
+            q, h = n // 2, n % 2
+            if h == 0:
+                gT_ps = psum_g.tile([P, PACK, 2 * P], BF16)
+                gT_tiles[q] = gT_ps
+            for j in range(PACK):
+                turn_bf16(gT_tiles[q][:, j, h * P : (h + 1) * P], g_tiles[q][:, h, j * P : (j + 1) * P], n < 3)
 
         def tanh(n):
             th = work.tile([P, P, PACK], F32)
@@ -159,29 +192,34 @@ def tile_oddlayer_t_v_kernel(
                 in1=sq_tiles[n][:], op0=ALU.is_le, op1=ALU.subtract,
             )
 
-        def times_g(q):
-            dz2 = work.tile([P, 2 * P, PACK], BF16, align_bytes=64)
+        def times_g(q, lo=0, hi=2):
+            if lo == 0:
+                dz2 = work.tile([P, 2 * P, PACK], BF16, align_bytes=64)
+                dz2_tiles[q] = dz2
+            cols = slice(lo * P, hi * P)
             nc.vector.scalar_tensor_tensor(
-                out=dz2[:], in0=slope_tiles[q][:].rearrange("p h n j -> p (h n) j"), scalar=0.0,
-                in1=gT_tiles[q][:].rearrange("p j m -> p m j"), op0=ALU.max, op1=ALU.mult,
+                out=dz2_tiles[q][:, cols, :], in0=slope_tiles[q][:, lo:hi].rearrange("p h n j -> p (h n) j"), scalar=0.0,
+                in1=gT_tiles[q][:, :, cols].rearrange("p j m -> p m j"), op0=ALU.max, op1=ALU.mult,
             )
-            dz2_tiles[q] = dz2
 
-        def quantise(q):
-            dz_codes = work.tile([P, 2 * P], U32, align_bytes=64)
-            dz_scales = work.tile([P, 2 * P], U8, align_bytes=64)
+        def quantise(q, lo=0, hi=2):
+            if lo == 0:
+                dz_codes = work.tile([P, 2 * P], U32, align_bytes=64)
+                dz_scales = work.tile([P, 2 * P], U8, align_bytes=64)
+                code_tiles[q] = (dz_codes, dz_scales)
+            cols = slice(lo * P, hi * P)
             nc.vector.quantize_mx(
-                out=dz_codes[:].bitcast(E5M2X4),
-                scales=dz_scales[:],
-                in_=dz2_tiles[q][:].rearrange("p m j -> p (m j)"),
+                out=code_tiles[q][0][:, cols].bitcast(E5M2X4),
+                scales=code_tiles[q][1][:, cols],
+                in_=dz2_tiles[q][:, cols, :].rearrange("p m j -> p (m j)"),
             )
-            code_tiles[q] = (dz_codes, dz_scales)
 
         def multiply(n):
             dz_codes, dz_scales = code_tiles[n // 2]
             cols = slice((n % 2) * P, (n % 2 + 1) * P)
             out_ps = psum_o.tile([P, FEATURES], F32)
-            nc.tensor.matmul_mx(
+            for again in range(2 if n < BLOCKS - 2 else 1):
+              nc.tensor.matmul_mx(
                 out=out_ps[:],
                 lhsT=dz_codes[:, cols].bitcast(E5M2X4),
                 lhsT_scale=dz_scales[:, cols],
@@ -196,45 +234,73 @@ def tile_oddlayer_t_v_kernel(
             if n % 2 == 0:
                 out_sb = out_pool.tile([P, 2, FEATURES], F32)
                 out_sb_tiles[n // 2] = out_sb
-            if through_vector(n):
+            if n == BLOCKS - 1:
+                half = FEATURES // 2
+                nc.vector.tensor_scalar_mul(out=out_sb_tiles[n // 2][:, 1, :half], in0=out_ps_tiles[n][:, :half], scalar1=0.5)
+                nc.scalar.mul(out=out_sb_tiles[n // 2][:, 1, half:], in_=out_ps_tiles[n][:, half:], mul=0.5)
+            elif through_vector(n):
                 nc.vector.tensor_scalar_mul(out=out_sb_tiles[n // 2][:, n % 2, :], in0=out_ps_tiles[n][:], scalar1=0.5)
             else:
                 nc.scalar.mul(out=out_sb_tiles[n // 2][:, n % 2, :], in_=out_ps_tiles[n][:], mul=0.5)
-            if n % 2 == 1:
+            if n >= BLOCKS - 2:
+                nc.sync.dma_start(out=out_view[n // 2][:, n % 2, :], in_=out_sb_tiles[n // 2][:, n % 2, :])
+            elif n % 2 == 1:
                 nc.sync.dma_start(out=out_view[n // 2], in_=out_sb_tiles[n // 2][:])
 
-        for s in range(-4, BLOCKS + 6):
+        absolute(0, slice(0, 1))
+        transpose_a(0)
+        absolute(0, slice(1, 2))
+        transpose_a(1)
+        keep_warm(2)
+        tanh(0)
+        mask_weights(0)
+        transpose_weights(0)
+        transpose_weights(1)
+        tanh(1)
+        square(0)
+        square(1)
+        absolute(1, slice(0, 2))
+        transpose_a(2)
+        group_weights(0)
+        group_weights(1)
+        transpose_g(0)
+        for s in range(BLOCKS + 4):
+            if s == BLOCKS - 1:
+                times_g(PAIRS - 1, 0, 1)
+            if s == BLOCKS:
+                times_g(PAIRS - 1, 1, 2)
+                quantise(PAIRS - 1, 1, 2)
             if is_block(s):
                 slope_of(s)
-            if s % 2 == 0 and is_block(s + 4):
-                absolute((s + 4) // 2)
-            if s % 2 == 1 and is_block(s - 3):
-                quantise((s - 3) // 2)
-            if s == -3:
-                mask_weights()
-            if s == ROW_BLOCKS:
+            if s == BLOCKS - 1:
+                quantise(PAIRS - 1, 0, 1)
+            if s == 0:
+                mask_weights(1)
+            if s % 2 == 0 and is_block(s - 2) and s < BLOCKS:
+                quantise((s - 2) // 2)
+            if s == 2:
                 quantise_weights()
-            if is_block(s - 5) and through_vector(s - 5):
-                leave_psum(s - 5)
-            if s % 2 == 0 and is_block(s - 2):
-                times_g((s - 2) // 2)
+            if s % 2 == 1 and is_block(s + 3):
+                absolute((s + 3) // 2, slice(0, 2))
+            if s % 2 == 1 and is_block(s) and s < BLOCKS - 1:
+                times_g(s // 2)
+            if is_block(s - 3) and through_vector(s - 3):
+                leave_psum(s - 3)
+            if is_block(s + 3):
+                transpose_a(s + 3)
+            if s == 0:
+                transpose_weights(2)
+                transpose_weights(3)
+            if is_block(s + 1):
+                transpose_g(s + 1)
+            if is_block(s - 2):
+                multiply(s - 2)
             if is_block(s + 2):
                 tanh(s + 2)
-            if is_row_block(s):
-                group_weights(s)
-            if is_block(s - 5) and not through_vector(s - 5):
-                leave_psum(s - 5)
+            if is_block(s - 3) and not through_vector(s - 3):
+                leave_psum(s - 3)
             if is_block(s + 2):
                 square(s + 2)
-            if s == -3:
-                transpose_weights()
-            if s % 2 == 0:
-                if is_block(s + 3):
-                    transpose_a(s + 3)
-                if is_block(s + 4):
-                    transpose_a(s + 4)
-                if is_block(s - 4):
-                    multiply(s - 4)
-                    multiply(s - 3)
-                if is_block(s + 2):
-                    transpose_g((s + 2) // 2)
+            if s == 1:
+                group_weights(2)
+                group_weights(3)

@@ -67,13 +67,13 @@ def tile_oddlayer_t_v_kernel(
             g_tiles.append(g_sb)
 
         load_z(0)
+        load_z(1)
         for h in range(2):
             rows = slice(2 * h, 2 * h + 2)
             nc.sync.dma_start(out=w_sb[:, rows, :], in_=w_view[:, rows, :])
             nc.sync.dma_start(out=m_sb[:, rows, :], in_=m_view[:, rows, :])
             if h == 0:
-                load_z(1)
-        load_g(0)
+                load_g(0)
         for q in range(2, PAIRS):
             load_z(q)
             load_g(q - 1)
@@ -151,6 +151,12 @@ def tile_oddlayer_t_v_kernel(
                 out=a_tiles[q][:, h, :].bitcast(I32), in_=z_tiles[q][:, h, :].bitcast(I32), scalar=0x7FFFFFFF, op=ALU.bitwise_and
             )
 
+        def transpose_z0():
+            zT_ps = psum_g.tile([P, PACK, P], F32, tag="gT_ps")
+            for j in range(PACK):
+                nc.tensor.transpose(zT_ps[:, j, :], z_tiles[0][:, 0, j * P : (j + 1) * P], ident_f32[:])
+            aT_tiles["z0"] = zT_ps
+
         def transpose_a(n):
             aT_ps = psum_a.tile([P, PACK, P], F32)
             for j in range(PACK):
@@ -174,7 +180,7 @@ def tile_oddlayer_t_v_kernel(
         def tanh(n):
             th = work.tile([P, P, PACK], F32)
             nc.scalar.activation(
-                out=th[:], in_=aT_tiles[n][:].rearrange("p j n -> p n j"), func=ACT.Tanh, scale=0.5
+                out=th[:], in_=aT_tiles["z0" if n == 0 else n][:].rearrange("p j n -> p n j"), func=ACT.Tanh, scale=0.5
             )
             th_tiles[n] = th
 
@@ -247,23 +253,18 @@ def tile_oddlayer_t_v_kernel(
             elif n % 2 == 1:
                 nc.sync.dma_start(out=out_view[n // 2], in_=out_sb_tiles[n // 2][:])
 
+        transpose_z0()
         absolute(0, slice(0, 1))
-        transpose_a(0)
         absolute(0, slice(1, 2))
+        transpose_a(0)
         transpose_a(1)
         keep_warm(2)
         tanh(0)
-        mask_weights(0)
-        transpose_weights(0)
-        transpose_weights(1)
-        tanh(1)
         square(0)
-        square(1)
+        tanh(1)
         absolute(1, slice(0, 2))
+        square(1)
         transpose_a(2)
-        group_weights(0)
-        group_weights(1)
-        transpose_g(0)
         for s in range(BLOCKS + 4):
             if s == BLOCKS - 1:
                 times_g(PAIRS - 1, 0, 1)
@@ -274,33 +275,42 @@ def tile_oddlayer_t_v_kernel(
                 slope_of(s)
             if s == BLOCKS - 1:
                 quantise(PAIRS - 1, 0, 1)
-            if s == 0:
-                mask_weights(1)
+            if s < 2:
+                mask_weights(s)
             if s % 2 == 0 and is_block(s - 2) and s < BLOCKS:
                 quantise((s - 2) // 2)
             if s == 2:
                 quantise_weights()
+            if s == 1:
+                times_g(0)
             if s % 2 == 1 and is_block(s + 3):
                 absolute((s + 3) // 2, slice(0, 2))
-            if s % 2 == 1 and is_block(s) and s < BLOCKS - 1:
+            if s % 2 == 1 and 1 < s < BLOCKS - 1:
                 times_g(s // 2)
             if is_block(s - 3) and through_vector(s - 3):
                 leave_psum(s - 3)
-            if is_block(s + 3):
-                transpose_a(s + 3)
             if s == 0:
-                transpose_weights(2)
-                transpose_weights(3)
-            if is_block(s + 1):
-                transpose_g(s + 1)
-            if is_block(s - 2):
-                multiply(s - 2)
+                transpose_a(3)
+                transpose_weights(0)
+                transpose_weights(1)
+                transpose_g(0)
+                transpose_g(1)
+            else:
+                if s == 1:
+                    transpose_weights(2)
+                    transpose_weights(3)
+                if is_block(s + 3):
+                    transpose_a(s + 3)
+                if is_block(s + 1):
+                    transpose_g(s + 1)
+                if is_block(s - 2):
+                    multiply(s - 2)
             if is_block(s + 2):
                 tanh(s + 2)
             if is_block(s - 3) and not through_vector(s - 3):
                 leave_psum(s - 3)
             if is_block(s + 2):
                 square(s + 2)
-            if s == 1:
-                group_weights(2)
-                group_weights(3)
+            if s < 2:
+                group_weights(2 * s)
+                group_weights(2 * s + 1)

@@ -224,7 +224,7 @@ def tile_oddlayer_t_v_kernel(
             dz_codes, dz_scales = code_tiles[n // 2]
             cols = slice((n % 2) * P, (n % 2 + 1) * P)
             out_ps = psum_o.tile([P, FEATURES], F32)
-            for again in range(2 if n < BLOCKS - 2 else 1):
+            for again in range(1):
               nc.tensor.matmul_mx(
                 out=out_ps[:],
                 lhsT=dz_codes[:, cols].bitcast(E5M2X4),
@@ -295,16 +295,23 @@ def tile_oddlayer_t_v_kernel(
                 transpose_weights(1)
                 transpose_g(0)
                 transpose_g(1)
-            else:
-                if s == 1:
-                    transpose_weights(2)
-                    transpose_weights(3)
-                if is_block(s + 3):
-                    transpose_a(s + 3)
-                if is_block(s + 1):
-                    transpose_g(s + 1)
-                if is_block(s - 2):
-                    multiply(s - 2)
+            elif s == 1:
+                transpose_weights(2)
+                transpose_weights(3)
+                transpose_a(4)
+                transpose_a(5)
+                transpose_g(2)
+                transpose_g(3)
+            elif s % 2 == 1:
+                for n in (s - 3, s - 2):
+                    if is_block(n):
+                        multiply(n)
+                for n in (s + 3, s + 4):
+                    if is_block(n):
+                        transpose_a(n)
+                for n in (s + 1, s + 2):
+                    if is_block(n):
+                        transpose_g(n)
             if is_block(s + 2):
                 tanh(s + 2)
             if is_block(s - 3) and not through_vector(s - 3):

@@ -35,7 +35,7 @@ def tile_oddlayer_t_v_kernel(
         consts = stack.enter_context(tc.tile_pool(name="consts", bufs=1))
         z_pool = stack.enter_context(tc.tile_pool(name="z_pool", bufs=PAIRS))
         g_pool = stack.enter_context(tc.tile_pool(name="g_pool", bufs=PAIRS))
-        work = stack.enter_context(tc.tile_pool(name="work", bufs=4))
+        work = stack.enter_context(tc.tile_pool(name="work", bufs=5))
         out_pool = stack.enter_context(tc.tile_pool(name="out_pool", bufs=10))
         psum_a = stack.enter_context(tc.psum_pool(name="psum_a", bufs=4))
         psum_g = stack.enter_context(tc.psum_pool(name="psum_g", bufs=2))
@@ -117,7 +117,7 @@ def tile_oddlayer_t_v_kernel(
             return 0 <= r < ROW_BLOCKS
 
         def through_vector(n):
-            return n % 8 == 7 and n < BLOCKS - 4
+            return False
 
         def mask_weights(half):
             rows = slice(2 * half, 2 * half + 2)
@@ -186,7 +186,12 @@ def tile_oddlayer_t_v_kernel(
 
         def square(n):
             sq = work.tile([P, P, PACK], F32)
-            nc.scalar.activation(out=sq[:], in_=th_tiles[n][:], func=ACT.Square)
+            if n % 2 == 1 and n > 4:
+                for c in range(1):
+                    part = slice(c * P // 1, (c + 1) * P // 1)
+                    nc.gpsimd.tensor_tensor(out=sq[:, part, :], in0=th_tiles[n][:, part, :], in1=th_tiles[n][:, part, :], op=ALU.mult)
+            else:
+                nc.scalar.activation(out=sq[:], in_=th_tiles[n][:], func=ACT.Square)
             sq_tiles[n] = sq
 
         def slope_of(n):

@@ -18,6 +18,7 @@ PACK = 4
 TOKENS = 4096
 FEATURES = 512
 CLIP = 10.0
+PUSH = 1024.0
 BLOCKS = TOKENS // P
 PAIRS = BLOCKS // 2
 ROW_BLOCKS = FEATURES // P
@@ -36,7 +37,7 @@ def tile_oddlayer_t_v_kernel(
         z_pool = stack.enter_context(tc.tile_pool(name="z_pool", bufs=PAIRS))
         g_pool = stack.enter_context(tc.tile_pool(name="g_pool", bufs=PAIRS))
         work = stack.enter_context(tc.tile_pool(name="work", bufs=5))
-        out_pool = stack.enter_context(tc.tile_pool(name="out_pool", bufs=10))
+        out_pool = stack.enter_context(tc.tile_pool(name="out_pool", bufs=9))
         psum_a = stack.enter_context(tc.psum_pool(name="psum_a", bufs=4))
         psum_g = stack.enter_context(tc.psum_pool(name="psum_g", bufs=2))
         psum_o = stack.enter_context(tc.psum_pool(name="psum_o", bufs=2))
@@ -92,19 +93,18 @@ def tile_oddlayer_t_v_kernel(
                 junk = psum_o.tile([P, FEATURES], F32, tag="out_ps")
                 nc.tensor.matmul(out=junk[:], lhsT=warm[:, :P], rhs=warm[:], start=True, stop=True)
 
-        keep_warm(3)
-
         wm_sb = consts.tile([P, ROW_BLOCKS, FEATURES], BF16)
         wm_grouped = consts.tile([P, FEATURES, PACK], BF16, align_bytes=64)
         wm_codes = consts.tile([P, FEATURES], U32, align_bytes=64)
         wm_scales = consts.tile([P, FEATURES], U8, align_bytes=64)
         wmT_tiles = {}
         a_tiles = {}
+        e_tiles = {}
         aT_tiles = {}
         gT_tiles = {}
         th_tiles = {}
         sq_tiles = {}
-        slope_tiles = {}
+        m_tiles = {}
         dz2_tiles = {}
         code_tiles = {}
         out_ps_tiles = {}
@@ -113,11 +113,24 @@ def tile_oddlayer_t_v_kernel(
         def is_block(n):
             return 0 <= n < BLOCKS
 
-        def is_row_block(r):
-            return 0 <= r < ROW_BLOCKS
+        def is_pair(q):
+            return 0 <= q < PAIRS
+
+        def pushed(n):
+            q = n // 2
+            return n % 2 == 0 and (False)
+
+        def square_on_gpsimd(n):
+            return n % 2 == 1 and 6 <= n < 32
 
         def through_vector(n):
             return False
+
+        def turn_bf16(out_ps, in_sb, as_matmul):
+            if as_matmul:
+                nc.tensor.matmul(out=out_ps, lhsT=in_sb, rhs=ident_bf16[:], start=True, stop=True)
+            else:
+                nc.tensor.transpose(out_ps, in_sb, ident_bf16[:])
 
         def mask_weights(half):
             rows = slice(2 * half, 2 * half + 2)
@@ -143,31 +156,46 @@ def tile_oddlayer_t_v_kernel(
                 in_=wm_grouped[:].rearrange("p i j -> p (i j)"),
             )
 
-        def absolute(q, h):
-            if q not in a_tiles:
+        def absolute(q, lo=0, hi=2):
+            if lo == 0:
                 a_sb = work.tile([P, 2, FEATURES], F32)
                 a_tiles[q] = a_sb
             nc.vector.tensor_single_scalar(
-                out=a_tiles[q][:, h, :].bitcast(I32), in_=z_tiles[q][:, h, :].bitcast(I32), scalar=0x7FFFFFFF, op=ALU.bitwise_and
+                out=a_tiles[q][:, lo:hi, :].bitcast(I32), in_=z_tiles[q][:, lo:hi, :].bitcast(I32),
+                scalar=0x7FFFFFFF, op=ALU.bitwise_and,
             )
+
+        def push_of(n):
+            if not pushed(n):
+                return
+            e_sb = work.tile([P, FEATURES], F32)
+            nc.vector.tensor_scalar(
+                out=e_sb[:], in0=a_tiles[n // 2][:, n % 2, :], scalar1=CLIP, scalar2=PUSH, op0=ALU.is_gt, op1=ALU.mult
+            )
+            e_tiles[n] = e_sb
+
+        def transpose_a(n):
+            aT_ps = psum_a.tile([P, PACK, P], F32)
+            for j in range(PACK):
+                cols = slice(j * P, (j + 1) * P)
+                if pushed(n):
+                    nc.tensor.matmul(
+                        out=aT_ps[:, j, :], lhsT=a_tiles[n // 2][:, n % 2, cols], rhs=ident_f32[:],
+                        is_transpose=True, start=True, stop=False,
+                    )
+                    nc.tensor.matmul(
+                        out=aT_ps[:, j, :], lhsT=e_tiles[n][:, cols], rhs=ident_f32[:],
+                        is_transpose=True, start=False, stop=True,
+                    )
+                else:
+                    nc.tensor.transpose(aT_ps[:, j, :], a_tiles[n // 2][:, n % 2, cols], ident_f32[:])
+            aT_tiles[n] = aT_ps
 
         def transpose_z0():
             zT_ps = psum_g.tile([P, PACK, P], F32, tag="gT_ps")
             for j in range(PACK):
                 nc.tensor.transpose(zT_ps[:, j, :], z_tiles[0][:, 0, j * P : (j + 1) * P], ident_f32[:])
             aT_tiles["z0"] = zT_ps
-
-        def transpose_a(n):
-            aT_ps = psum_a.tile([P, PACK, P], F32)
-            for j in range(PACK):
-                nc.tensor.transpose(aT_ps[:, j, :], a_tiles[n // 2][:, n % 2, j * P : (j + 1) * P], ident_f32[:])
-            aT_tiles[n] = aT_ps
-
-        def turn_bf16(out_ps, in_sb, as_matmul):
-            if as_matmul:
-                nc.tensor.matmul(out=out_ps, lhsT=in_sb, rhs=ident_bf16[:], start=True, stop=True)
-            else:
-                nc.tensor.transpose(out_ps, in_sb, ident_bf16[:])
 
         def transpose_g(n):
             q, h = n // 2, n % 2
@@ -185,22 +213,26 @@ def tile_oddlayer_t_v_kernel(
             th_tiles[n] = th
 
         def square(n):
-            sq = work.tile([P, P, PACK], F32)
-            if n % 2 == 1 and n > 4:
-                for c in range(1):
-                    part = slice(c * P // 1, (c + 1) * P // 1)
-                    nc.gpsimd.tensor_tensor(out=sq[:, part, :], in0=th_tiles[n][:, part, :], in1=th_tiles[n][:, part, :], op=ALU.mult)
+            if n // 2 not in m_tiles:
+                m_sb = work.tile([P, 2, P, PACK], F32)
+                m_tiles[n // 2] = m_sb
+            if pushed(n):
+                sq = m_tiles[n // 2][:, n % 2]
             else:
-                nc.scalar.activation(out=sq[:], in_=th_tiles[n][:], func=ACT.Square)
+                sq_sb = work.tile([P, P, PACK], F32)
+                sq = sq_sb[:]
+            if square_on_gpsimd(n):
+                nc.gpsimd.tensor_tensor(out=sq, in0=th_tiles[n][:], in1=th_tiles[n][:], op=ALU.mult)
+            else:
+                nc.scalar.activation(out=sq, in_=th_tiles[n][:], func=ACT.Square)
             sq_tiles[n] = sq
 
-        def slope_of(n):
-            if n % 2 == 0:
-                slope = work.tile([P, 2, P, PACK], F32)
-                slope_tiles[n // 2] = slope
+        def clip_of(n):
+            if pushed(n):
+                return
             nc.vector.scalar_tensor_tensor(
-                out=slope_tiles[n // 2][:, n % 2], in0=aT_tiles[n][:].rearrange("p j n -> p n j"), scalar=CLIP,
-                in1=sq_tiles[n][:], op0=ALU.is_le, op1=ALU.subtract,
+                out=m_tiles[n // 2][:, n % 2], in0=aT_tiles[n][:].rearrange("p j n -> p n j"), scalar=CLIP,
+                in1=sq_tiles[n], op0=ALU.is_gt, op1=ALU.max,
             )
 
         def times_g(q, lo=0, hi=2):
@@ -209,8 +241,8 @@ def tile_oddlayer_t_v_kernel(
                 dz2_tiles[q] = dz2
             cols = slice(lo * P, hi * P)
             nc.vector.scalar_tensor_tensor(
-                out=dz2_tiles[q][:, cols, :], in0=slope_tiles[q][:, lo:hi].rearrange("p h n j -> p (h n) j"), scalar=0.0,
-                in1=gT_tiles[q][:, :, cols].rearrange("p j m -> p m j"), op0=ALU.max, op1=ALU.mult,
+                out=dz2_tiles[q][:, cols, :], in0=m_tiles[q][:, lo:hi].rearrange("p h n j -> p (h n) j"), scalar=1.0,
+                in1=gT_tiles[q][:, :, cols].rearrange("p j m -> p m j"), op0=ALU.subtract, op1=ALU.mult,
             )
 
         def quantise(q, lo=0, hi=2):
@@ -230,15 +262,15 @@ def tile_oddlayer_t_v_kernel(
             cols = slice((n % 2) * P, (n % 2 + 1) * P)
             out_ps = psum_o.tile([P, FEATURES], F32)
             for again in range(1):
-              nc.tensor.matmul_mx(
-                out=out_ps[:],
-                lhsT=dz_codes[:, cols].bitcast(E5M2X4),
-                lhsT_scale=dz_scales[:, cols],
-                rhs=wm_codes[:].bitcast(E4M3X4),
-                rhs_scale=wm_scales[:],
-                start=True,
-                stop=True,
-            )
+                nc.tensor.matmul_mx(
+                    out=out_ps[:],
+                    lhsT=dz_codes[:, cols].bitcast(E5M2X4),
+                    lhsT_scale=dz_scales[:, cols],
+                    rhs=wm_codes[:].bitcast(E4M3X4),
+                    rhs_scale=wm_scales[:],
+                    start=True,
+                    stop=True,
+                )
             out_ps_tiles[n] = out_ps
 
         def leave_psum(n):
@@ -247,82 +279,96 @@ def tile_oddlayer_t_v_kernel(
                 out_sb_tiles[n // 2] = out_sb
             if n == BLOCKS - 1:
                 half = FEATURES // 2
-                nc.vector.tensor_scalar_mul(out=out_sb_tiles[n // 2][:, 1, :half], in0=out_ps_tiles[n][:, :half], scalar1=0.5)
-                nc.scalar.mul(out=out_sb_tiles[n // 2][:, 1, half:], in_=out_ps_tiles[n][:, half:], mul=0.5)
+                nc.vector.tensor_scalar_mul(out=out_sb_tiles[n // 2][:, 1, :half], in0=out_ps_tiles[n][:, :half], scalar1=-0.5)
+                nc.scalar.mul(out=out_sb_tiles[n // 2][:, 1, half:], in_=out_ps_tiles[n][:, half:], mul=-0.5)
             elif through_vector(n):
-                nc.vector.tensor_scalar_mul(out=out_sb_tiles[n // 2][:, n % 2, :], in0=out_ps_tiles[n][:], scalar1=0.5)
+                nc.vector.tensor_scalar_mul(out=out_sb_tiles[n // 2][:, n % 2, :], in0=out_ps_tiles[n][:], scalar1=-0.5)
             else:
-                nc.scalar.mul(out=out_sb_tiles[n // 2][:, n % 2, :], in_=out_ps_tiles[n][:], mul=0.5)
-            if n >= BLOCKS - 2:
-                nc.sync.dma_start(out=out_view[n // 2][:, n % 2, :], in_=out_sb_tiles[n // 2][:, n % 2, :])
+                nc.scalar.mul(out=out_sb_tiles[n // 2][:, n % 2, :], in_=out_ps_tiles[n][:], mul=-0.5)
+            if n == BLOCKS - 1:
+                for cols in (slice(0, FEATURES // 2), slice(FEATURES // 2, FEATURES)):
+                    nc.sync.dma_start(out=out_view[n // 2][:, 1, cols], in_=out_sb_tiles[n // 2][:, 1, cols])
+            elif n == BLOCKS - 2:
+                nc.sync.dma_start(out=out_view[n // 2][:, 0, :], in_=out_sb_tiles[n // 2][:, 0, :])
             elif n % 2 == 1:
                 nc.sync.dma_start(out=out_view[n // 2], in_=out_sb_tiles[n // 2][:])
 
+        keep_warm(3)
         transpose_z0()
-        absolute(0, slice(0, 1))
-        absolute(0, slice(1, 2))
+        absolute(0, 0, 1)
+        absolute(0, 1, 2)
         transpose_a(0)
         transpose_a(1)
         keep_warm(2)
         tanh(0)
         square(0)
         tanh(1)
-        absolute(1, slice(0, 2))
         square(1)
+        absolute(1)
         transpose_a(2)
-        for s in range(BLOCKS + 4):
-            if s == BLOCKS - 1:
-                times_g(PAIRS - 1, 0, 1)
-            if s == BLOCKS:
-                times_g(PAIRS - 1, 1, 2)
-                quantise(PAIRS - 1, 1, 2)
-            if is_block(s):
-                slope_of(s)
-            if s == BLOCKS - 1:
-                quantise(PAIRS - 1, 0, 1)
-            if s < 2:
-                mask_weights(s)
-            if s % 2 == 0 and is_block(s - 2) and s < BLOCKS:
-                quantise((s - 2) // 2)
-            if s == 2:
+        transpose_a(3)
+        clip_of(0)
+        mask_weights(0)
+        transpose_g(0)
+        transpose_g(1)
+        tanh(2)
+        square(2)
+        transpose_weights(0)
+        transpose_weights(1)
+        clip_of(1)
+        mask_weights(1)
+        times_g(0)
+        absolute(2)
+        tanh(3)
+        group_weights(0)
+        group_weights(1)
+        square(3)
+        transpose_weights(2)
+        transpose_weights(3)
+        transpose_a(5)
+        transpose_a(4)
+        transpose_g(2)
+        transpose_g(3)
+        group_weights(2)
+        group_weights(3)
+        tanh(4)
+        tanh(5)
+        square(5)
+        square(4)
+        for q in range(1, PAIRS + 1):
+            last = q == PAIRS - 1
+            if is_pair(q):
+                clip_of(2 * q)
+            if q < PAIRS - 2 or last:
+                quantise(q - 1)
+            if last:
+                times_g(q, 0, 1)
+            if is_pair(q):
+                clip_of(2 * q + 1)
+            if q == PAIRS - 2:
+                quantise(q - 1)
+            if last:
+                quantise(q, 0, 1)
+                times_g(q, 1, 2)
+                quantise(q, 1, 2)
+            if q == 1:
                 quantise_weights()
-            if s == 1:
-                times_g(0)
-            if s % 2 == 1 and is_block(s + 3):
-                absolute((s + 3) // 2, slice(0, 2))
-            if s % 2 == 1 and 1 < s < BLOCKS - 1:
-                times_g(s // 2)
-            if is_block(s - 3) and through_vector(s - 3):
-                leave_psum(s - 3)
-            if s == 0:
-                transpose_a(3)
-                transpose_weights(0)
-                transpose_weights(1)
-                transpose_g(0)
-                transpose_g(1)
-            elif s == 1:
-                transpose_weights(2)
-                transpose_weights(3)
-                transpose_a(4)
-                transpose_a(5)
-                transpose_g(2)
-                transpose_g(3)
-            elif s % 2 == 1:
-                for n in (s - 3, s - 2):
-                    if is_block(n):
-                        multiply(n)
-                for n in (s + 3, s + 4):
-                    if is_block(n):
-                        transpose_a(n)
-                for n in (s + 1, s + 2):
-                    if is_block(n):
-                        transpose_g(n)
-            if is_block(s + 2):
-                tanh(s + 2)
-            if is_block(s - 3) and not through_vector(s - 3):
-                leave_psum(s - 3)
-            if is_block(s + 2):
-                square(s + 2)
-            if s < 2:
-                group_weights(2 * s)
-                group_weights(2 * s + 1)
+            if is_pair(q + 2):
+                absolute(q + 2)
+            if is_pair(q) and not last:
+                times_g(q)
+            multiply(2 * q - 2)
+            multiply(2 * q - 1)
+            if is_pair(q + 2):
+                transpose_a(2 * q + 5)
+                transpose_a(2 * q + 4)
+            if is_pair(q + 1):
+                transpose_g(2 * q + 2)
+                transpose_g(2 * q + 3)
+            if q > 1 and is_pair(q + 1):
+                tanh(2 * q + 2)
+                tanh(2 * q + 3)
+                square(2 * q + 3)
+                square(2 * q + 2)
+            leave_psum(2 * q - 2)
+            leave_psum(2 * q - 1)

@@ -85,13 +85,13 @@ def tile_oddlayer_t_v_kernel(
         ident_bf16 = consts.tile([P, P], BF16)
         make_identity(nc, ident_bf16[:])
 
-        warm = consts.tile([P, FEATURES], BF16)
+        warm = consts.tile([P, P], F32)
         nc.vector.memset(warm[:], 0.0)
 
         def keep_warm(passes):
             for i in range(passes):
-                junk = psum_o.tile([P, FEATURES], F32, tag="out_ps")
-                nc.tensor.matmul(out=junk[:], lhsT=warm[:, :P], rhs=warm[:], start=True, stop=True)
+                junk = psum_o.tile([P, P], F32, tag="out_ps")
+                nc.tensor.matmul(out=junk[:], lhsT=warm[:], rhs=warm[:], start=True, stop=True)
 
         wm_sb = consts.tile([P, ROW_BLOCKS, FEATURES], BF16)
         wm_grouped = consts.tile([P, FEATURES, PACK], BF16, align_bytes=64)
@@ -118,7 +118,7 @@ def tile_oddlayer_t_v_kernel(
 
         def pushed(n):
             q = n // 2
-            return n % 2 == 0 and (False)
+            return n % 2 == 0 and (3 <= q)
 
         def square_on_gpsimd(n):
             return n % 2 == 1 and 6 <= n < 32
@@ -185,7 +185,7 @@ def tile_oddlayer_t_v_kernel(
                     )
                     nc.tensor.matmul(
                         out=aT_ps[:, j, :], lhsT=e_tiles[n][:, cols], rhs=ident_f32[:],
-                        is_transpose=True, start=False, stop=True,
+                        is_transpose=j >= 1, start=False, stop=True,
                     )
                 else:
                     nc.tensor.transpose(aT_ps[:, j, :], a_tiles[n // 2][:, n % 2, cols], ident_f32[:])
@@ -293,7 +293,7 @@ def tile_oddlayer_t_v_kernel(
             elif n % 2 == 1:
                 nc.sync.dma_start(out=out_view[n // 2], in_=out_sb_tiles[n // 2][:])
 
-        keep_warm(3)
+        keep_warm(5)
         transpose_z0()
         absolute(0, 0, 1)
         absolute(0, 1, 2)
@@ -357,18 +357,31 @@ def tile_oddlayer_t_v_kernel(
                 absolute(q + 2)
             if is_pair(q) and not last:
                 times_g(q)
+            if is_pair(q + 2):
+                push_of(2 * q + 4)
             multiply(2 * q - 2)
             multiply(2 * q - 1)
             if is_pair(q + 2):
                 transpose_a(2 * q + 5)
-                transpose_a(2 * q + 4)
             if is_pair(q + 1):
                 transpose_g(2 * q + 2)
                 transpose_g(2 * q + 3)
-            if q > 1 and is_pair(q + 1):
+            if is_pair(q + 2):
+                transpose_a(2 * q + 4)
+            if q > 1 and is_pair(q + 1) and not pushed(2 * q + 2):
                 tanh(2 * q + 2)
                 tanh(2 * q + 3)
                 square(2 * q + 3)
                 square(2 * q + 2)
-            leave_psum(2 * q - 2)
-            leave_psum(2 * q - 1)
+                leave_psum(2 * q - 2)
+                leave_psum(2 * q - 1)
+            elif q > 1 and is_pair(q + 1):
+                tanh(2 * q + 3)
+                square(2 * q + 3)
+                tanh(2 * q + 2)
+                leave_psum(2 * q - 2)
+                square(2 * q + 2)
+                leave_psum(2 * q - 1)
+            else:
+                leave_psum(2 * q - 2)
+                leave_psum(2 * q - 1)

@@ -37,7 +37,7 @@ def tile_oddlayer_t_v_kernel(
         z_pool = stack.enter_context(tc.tile_pool(name="z_pool", bufs=PAIRS))
         g_pool = stack.enter_context(tc.tile_pool(name="g_pool", bufs=PAIRS))
         work = stack.enter_context(tc.tile_pool(name="work", bufs=5))
-        out_pool = stack.enter_context(tc.tile_pool(name="out_pool", bufs=9))
+        out_pool = stack.enter_context(tc.tile_pool(name="out_pool", bufs=8))
         psum_a = stack.enter_context(tc.psum_pool(name="psum_a", bufs=4))
         psum_g = stack.enter_context(tc.psum_pool(name="psum_g", bufs=2))
         psum_o = stack.enter_context(tc.psum_pool(name="psum_o", bufs=2))
@@ -92,6 +92,8 @@ def tile_oddlayer_t_v_kernel(
             for i in range(passes):
                 junk = psum_o.tile([P, P], F32, tag="out_ps")
                 nc.tensor.matmul(out=junk[:], lhsT=warm[:], rhs=warm[:], start=True, stop=True)
+
+        warm32 = warm
 
         wm_sb = consts.tile([P, ROW_BLOCKS, FEATURES], BF16)
         wm_grouped = consts.tile([P, FEATURES, PACK], BF16, align_bytes=64)
@@ -165,10 +167,13 @@ def tile_oddlayer_t_v_kernel(
                 scalar=0x7FFFFFFF, op=ALU.bitwise_and,
             )
 
+        def mask_bf16(n):
+            return n % 4 == 2
+
         def push_of(n):
             if not pushed(n):
                 return
-            e_sb = work.tile([P, FEATURES], F32)
+            e_sb = work.tile([P, FEATURES], BF16 if mask_bf16(n) else F32, tag="e_bf" if mask_bf16(n) else "e_f32")
             nc.vector.tensor_scalar(
                 out=e_sb[:], in0=a_tiles[n // 2][:, n % 2, :], scalar1=CLIP, scalar2=PUSH, op0=ALU.is_gt, op1=ALU.mult
             )
@@ -183,10 +188,13 @@ def tile_oddlayer_t_v_kernel(
                         out=aT_ps[:, j, :], lhsT=a_tiles[n // 2][:, n % 2, cols], rhs=ident_f32[:],
                         is_transpose=True, start=True, stop=False,
                     )
-                    nc.tensor.matmul(
-                        out=aT_ps[:, j, :], lhsT=e_tiles[n][:, cols], rhs=ident_f32[:],
-                        is_transpose=j >= 1, start=False, stop=True,
-                    )
+                    if mask_bf16(n):
+                        nc.tensor.matmul(out=aT_ps[:, j, :], lhsT=e_tiles[n][:, cols], rhs=ident_bf16[:], start=False, stop=True)
+                    else:
+                        nc.tensor.matmul(
+                            out=aT_ps[:, j, :], lhsT=e_tiles[n][:, cols], rhs=ident_f32[:],
+                            is_transpose=True, start=False, stop=True,
+                        )
                 else:
                     nc.tensor.transpose(aT_ps[:, j, :], a_tiles[n // 2][:, n % 2, cols], ident_f32[:])
             aT_tiles[n] = aT_ps
@@ -203,7 +211,7 @@ def tile_oddlayer_t_v_kernel(
                 gT_ps = psum_g.tile([P, PACK, 2 * P], BF16)
                 gT_tiles[q] = gT_ps
             for j in range(PACK):
-                turn_bf16(gT_tiles[q][:, j, h * P : (h + 1) * P], g_tiles[q][:, h, j * P : (j + 1) * P], n < 3)
+                turn_bf16(gT_tiles[q][:, j, h * P : (h + 1) * P], g_tiles[q][:, h, j * P : (j + 1) * P], False)
 
         def tanh(n):
             th = work.tile([P, P, PACK], F32)
@@ -293,13 +301,13 @@ def tile_oddlayer_t_v_kernel(
             elif n % 2 == 1:
                 nc.sync.dma_start(out=out_view[n // 2], in_=out_sb_tiles[n // 2][:])
 
-        keep_warm(5)
+        keep_warm(3)
         transpose_z0()
         absolute(0, 0, 1)
         absolute(0, 1, 2)
         transpose_a(0)
         transpose_a(1)
-        keep_warm(2)
+        keep_warm(3)
         tanh(0)
         square(0)
         tanh(1)

@@ -120,13 +120,10 @@ def tile_oddlayer_t_v_kernel(
 
         def pushed(n):
             q = n // 2
-            return n % 2 == 0 and (3 <= q)
+            return n % 2 == 0 and (2 <= q)
 
         def square_on_gpsimd(n):
             return n % 2 == 1 and 6 <= n < 32
-
-        def through_vector(n):
-            return False
 
         def turn_bf16(out_ps, in_sb, as_matmul):
             if as_matmul:
@@ -286,17 +283,15 @@ def tile_oddlayer_t_v_kernel(
                 out_sb = out_pool.tile([P, 2, FEATURES], F32)
                 out_sb_tiles[n // 2] = out_sb
             if n == BLOCKS - 1:
-                half = FEATURES // 2
-                nc.vector.tensor_scalar_mul(out=out_sb_tiles[n // 2][:, 1, :half], in0=out_ps_tiles[n][:, :half], scalar1=-0.5)
-                nc.scalar.mul(out=out_sb_tiles[n // 2][:, 1, half:], in_=out_ps_tiles[n][:, half:], mul=-0.5)
-            elif through_vector(n):
-                nc.vector.tensor_scalar_mul(out=out_sb_tiles[n // 2][:, n % 2, :], in0=out_ps_tiles[n][:], scalar1=-0.5)
+                for cols in (slice(0, FEATURES // 2), slice(FEATURES // 2, FEATURES)):
+                    nc.scalar.mul(out=out_sb_tiles[n // 2][:, 1, cols], in_=out_ps_tiles[n][:, cols], mul=-0.5)
+                    nc.sync.dma_start(out=out_view[n // 2][:, 1, cols], in_=out_sb_tiles[n // 2][:, 1, cols])
+                return
+            if n == BLOCKS - 2:
+                nc.vector.tensor_scalar_mul(out=out_sb_tiles[n // 2][:, 0, :], in0=out_ps_tiles[n][:], scalar1=-0.5)
             else:
                 nc.scalar.mul(out=out_sb_tiles[n // 2][:, n % 2, :], in_=out_ps_tiles[n][:], mul=-0.5)
-            if n == BLOCKS - 1:
-                for cols in (slice(0, FEATURES // 2), slice(FEATURES // 2, FEATURES)):
-                    nc.sync.dma_start(out=out_view[n // 2][:, 1, cols], in_=out_sb_tiles[n // 2][:, 1, cols])
-            elif n == BLOCKS - 2:
+            if n == BLOCKS - 2:
                 nc.sync.dma_start(out=out_view[n // 2][:, 0, :], in_=out_sb_tiles[n // 2][:, 0, :])
             elif n % 2 == 1:
                 nc.sync.dma_start(out=out_view[n // 2], in_=out_sb_tiles[n // 2][:])
@@ -327,6 +322,8 @@ def tile_oddlayer_t_v_kernel(
         mask_weights(1)
         times_g(0)
         absolute(2)
+        clip_of(2)
+        push_of(4)
         tanh(3)
         group_weights(0)
         group_weights(1)
@@ -339,13 +336,13 @@ def tile_oddlayer_t_v_kernel(
         transpose_g(3)
         group_weights(2)
         group_weights(3)
-        tanh(4)
         tanh(5)
         square(5)
+        tanh(4)
         square(4)
         for q in range(1, PAIRS + 1):
             last = q == PAIRS - 1
-            if is_pair(q):
+            if is_pair(q) and q > 1:
                 clip_of(2 * q)
             if q < PAIRS - 2 or last:
                 quantise(q - 1)

@@ -284,13 +284,17 @@ def tile_oddlayer_t_v_kernel(
                 out_sb_tiles[n // 2] = out_sb
             if n == BLOCKS - 1:
                 for cols in (slice(0, FEATURES // 2), slice(FEATURES // 2, FEATURES)):
-                    nc.scalar.mul(out=out_sb_tiles[n // 2][:, 1, cols], in_=out_ps_tiles[n][:, cols], mul=-0.5)
+                    nc.scalar.activation(
+                        out=out_sb_tiles[n // 2][:, 1, cols], in_=out_ps_tiles[n][:, cols], func=ACT.Copy, scale=-0.5
+                    )
                     nc.sync.dma_start(out=out_view[n // 2][:, 1, cols], in_=out_sb_tiles[n // 2][:, 1, cols])
                 return
             if n == BLOCKS - 2:
                 nc.vector.tensor_scalar_mul(out=out_sb_tiles[n // 2][:, 0, :], in0=out_ps_tiles[n][:], scalar1=-0.5)
             else:
-                nc.scalar.mul(out=out_sb_tiles[n // 2][:, n % 2, :], in_=out_ps_tiles[n][:], mul=-0.5)
+                nc.scalar.activation(
+                    out=out_sb_tiles[n // 2][:, n % 2, :], in_=out_ps_tiles[n][:], func=ACT.Copy, scale=-0.5
+                )
             if n == BLOCKS - 2:
                 nc.sync.dma_start(out=out_view[n // 2][:, 0, :], in_=out_sb_tiles[n // 2][:, 0, :])
             elif n % 2 == 1:

@@ -93,8 +93,6 @@ def tile_oddlayer_t_v_kernel(
                 junk = psum_o.tile([P, P], F32, tag="out_ps")
                 nc.tensor.matmul(out=junk[:], lhsT=warm[:], rhs=warm[:], start=True, stop=True)
 
-        warm32 = warm
-
         wm_sb = consts.tile([P, ROW_BLOCKS, FEATURES], BF16)
         wm_grouped = consts.tile([P, FEATURES, PACK], BF16, align_bytes=64)
         wm_codes = consts.tile([P, FEATURES], U32, align_bytes=64)
@@ -123,7 +121,7 @@ def tile_oddlayer_t_v_kernel(
             return n % 2 == 0 and (2 <= q)
 
         def square_on_gpsimd(n):
-            return n % 2 == 1 and 6 <= n < 32
+            return n % 2 == 1 and 7 <= n < 32
 
         def turn_bf16(out_ps, in_sb, as_matmul):
             if as_matmul:
@@ -217,6 +215,10 @@ def tile_oddlayer_t_v_kernel(
             )
             th_tiles[n] = th
 
+        def wait_for_vector(q):
+            gate = work.tile([P, 1], F32)
+            nc.gpsimd.tensor_copy(out=gate[:], in_=a_tiles[q][:, 1, FEATURES - 1 : FEATURES])
+
         def square(n):
             if n // 2 not in m_tiles:
                 m_sb = work.tile([P, 2, P, PACK], F32)
@@ -265,17 +267,19 @@ def tile_oddlayer_t_v_kernel(
         def multiply(n):
             dz_codes, dz_scales = code_tiles[n // 2]
             cols = slice((n % 2) * P, (n % 2 + 1) * P)
-            out_ps = psum_o.tile([P, FEATURES], F32)
-            for again in range(1):
-                nc.tensor.matmul_mx(
-                    out=out_ps[:],
-                    lhsT=dz_codes[:, cols].bitcast(E5M2X4),
-                    lhsT_scale=dz_scales[:, cols],
-                    rhs=wm_codes[:].bitcast(E4M3X4),
-                    rhs_scale=wm_scales[:],
-                    start=True,
-                    stop=True,
-                )
+            if n >= BLOCKS - 2:
+                out_ps = psum_a.tile([P, FEATURES], F32, tag="aT_ps")
+            else:
+                out_ps = psum_o.tile([P, FEATURES], F32)
+            nc.tensor.matmul_mx(
+                out=out_ps[:],
+                lhsT=dz_codes[:, cols].bitcast(E5M2X4),
+                lhsT_scale=dz_scales[:, cols],
+                rhs=wm_codes[:].bitcast(E4M3X4),
+                rhs_scale=wm_scales[:],
+                start=True,
+                stop=True,
+            )
             out_ps_tiles[n] = out_ps
 
         def leave_psum(n):
@@ -284,19 +288,21 @@ def tile_oddlayer_t_v_kernel(
                 out_sb_tiles[n // 2] = out_sb
             if n == BLOCKS - 1:
                 for cols in (slice(0, FEATURES // 2), slice(FEATURES // 2, FEATURES)):
-                    nc.scalar.activation(
-                        out=out_sb_tiles[n // 2][:, 1, cols], in_=out_ps_tiles[n][:, cols], func=ACT.Copy, scale=-0.5
+                    nc.vector.tensor_scalar_mul(
+                        out=out_sb_tiles[n // 2][:, 1, cols], in0=out_ps_tiles[n][:, cols], scalar1=-0.5
                     )
                     nc.sync.dma_start(out=out_view[n // 2][:, 1, cols], in_=out_sb_tiles[n // 2][:, 1, cols])
                 return
-            if n == BLOCKS - 2:
-                nc.vector.tensor_scalar_mul(out=out_sb_tiles[n // 2][:, 0, :], in0=out_ps_tiles[n][:], scalar1=-0.5)
+            if n == BLOCKS - 3:
+                nc.vector.tensor_scalar_mul(
+                    out=out_sb_tiles[n // 2][:, n % 2, :], in0=out_ps_tiles[n][:], scalar1=-0.5
+                )
             else:
                 nc.scalar.activation(
                     out=out_sb_tiles[n // 2][:, n % 2, :], in_=out_ps_tiles[n][:], func=ACT.Copy, scale=-0.5
                 )
-            if n == BLOCKS - 2:
-                nc.sync.dma_start(out=out_view[n // 2][:, 0, :], in_=out_sb_tiles[n // 2][:, 0, :])
+            if n >= BLOCKS - 6:
+                nc.sync.dma_start(out=out_view[n // 2][:, n % 2, :], in_=out_sb_tiles[n // 2][:, n % 2, :])
             elif n % 2 == 1:
                 nc.sync.dma_start(out=out_view[n // 2], in_=out_sb_tiles[n // 2][:])
 
@@ -328,6 +334,7 @@ def tile_oddlayer_t_v_kernel(
         absolute(2)
         clip_of(2)
         push_of(4)
+        absolute(3)
         tanh(3)
         group_weights(0)
         group_weights(1)
@@ -346,50 +353,52 @@ def tile_oddlayer_t_v_kernel(
         square(4)
         for q in range(1, PAIRS + 1):
             last = q == PAIRS - 1
-            if is_pair(q) and q > 1:
-                clip_of(2 * q)
-            if q < PAIRS - 2 or last:
-                quantise(q - 1)
-            if last:
-                times_g(q, 0, 1)
-            if is_pair(q):
-                clip_of(2 * q + 1)
-            if q == PAIRS - 2:
-                quantise(q - 1)
-            if last:
-                quantise(q, 0, 1)
-                times_g(q, 1, 2)
-                quantise(q, 1, 2)
             if q == 1:
+                quantise(0)
+                clip_of(3)
+                push_of(6)
                 quantise_weights()
-            if is_pair(q + 2):
-                absolute(q + 2)
-            if is_pair(q) and not last:
-                times_g(q)
-            if is_pair(q + 2):
+                absolute(4)
+                times_g(1)
+            elif q < PAIRS - 2:
+                clip_of(2 * q + 1)
                 push_of(2 * q + 4)
-            multiply(2 * q - 2)
-            multiply(2 * q - 1)
+                quantise(q - 1)
+                if is_pair(q + 3):
+                    absolute(q + 3)
+                times_g(q)
+            elif q == PAIRS - 2:
+                clip_of(2 * q + 1)
+                times_g(q, 0, 1)
+                times_g(q, 1, 2)
+                quantise(q - 1)
+            elif last:
+                clip_of(2 * q + 1)
+                quantise(q - 1)
+                times_g(q, 0, 1)
+                times_g(q, 1, 2)
+                quantise(q, 0, 1)
+                quantise(q, 1, 2)
             if is_pair(q + 2):
                 transpose_a(2 * q + 5)
+                transpose_a(2 * q + 4)
+            if q < PAIRS - 3:
+                multiply(2 * q - 2)
+                multiply(2 * q - 1)
             if is_pair(q + 1):
                 transpose_g(2 * q + 2)
                 transpose_g(2 * q + 3)
+            if q >= PAIRS - 3:
+                multiply(2 * q - 2)
+                multiply(2 * q - 1)
             if is_pair(q + 2):
-                transpose_a(2 * q + 4)
-            if q > 1 and is_pair(q + 1) and not pushed(2 * q + 2):
-                tanh(2 * q + 2)
-                tanh(2 * q + 3)
-                square(2 * q + 3)
-                square(2 * q + 2)
+                tanh(2 * q + 5)
+                if square_on_gpsimd(2 * q + 5) and is_pair(q + 3):
+                    wait_for_vector(q + 3)
+                square(2 * q + 5)
+                tanh(2 * q + 4)
                 leave_psum(2 * q - 2)
-                leave_psum(2 * q - 1)
-            elif q > 1 and is_pair(q + 1):
-                tanh(2 * q + 3)
-                square(2 * q + 3)
-                tanh(2 * q + 2)
-                leave_psum(2 * q - 2)
-                square(2 * q + 2)
+                square(2 * q + 4)
                 leave_psum(2 * q - 1)
             else:
                 leave_psum(2 * q - 2)

@@ -271,15 +271,16 @@ def tile_oddlayer_t_v_kernel(
                 out_ps = psum_a.tile([P, FEATURES], F32, tag="aT_ps")
             else:
                 out_ps = psum_o.tile([P, FEATURES], F32)
-            nc.tensor.matmul_mx(
-                out=out_ps[:],
-                lhsT=dz_codes[:, cols].bitcast(E5M2X4),
-                lhsT_scale=dz_scales[:, cols],
-                rhs=wm_codes[:].bitcast(E4M3X4),
-                rhs_scale=wm_scales[:],
-                start=True,
-                stop=True,
-            )
+            for again in range(1 + n % 2):
+                nc.tensor.matmul_mx(
+                    out=out_ps[:],
+                    lhsT=dz_codes[:, cols].bitcast(E5M2X4),
+                    lhsT_scale=dz_scales[:, cols],
+                    rhs=wm_codes[:].bitcast(E4M3X4),
+                    rhs_scale=wm_scales[:],
+                    start=True,
+                    stop=True,
+                )
             out_ps_tiles[n] = out_ps
 
         def leave_psum(n):

@@ -175,7 +175,8 @@ def tile_oddlayer_t_v_kernel(
             e_tiles[n] = e_sb
 
         def transpose_a(n):
-            aT_ps = psum_a.tile([P, PACK, P], F32)
+            held = n % 2 == 1 or n == 0
+            aT_ps = psum_a.tile([P, PACK, P], F32, tag="held_ps" if held else "free_ps", bufs=3 if held else 1)
             for j in range(PACK):
                 cols = slice(j * P, (j + 1) * P)
                 if pushed(n):
@@ -215,16 +216,14 @@ def tile_oddlayer_t_v_kernel(
             )
             th_tiles[n] = th
 
-        def wait_for_vector(q):
-            gate = work.tile([P, 1], F32)
-            nc.gpsimd.tensor_copy(out=gate[:], in_=a_tiles[q][:, 1, FEATURES - 1 : FEATURES])
-
         def square(n):
             if n // 2 not in m_tiles:
                 m_sb = work.tile([P, 2, P, PACK], F32)
                 m_tiles[n // 2] = m_sb
             if pushed(n):
                 sq = m_tiles[n // 2][:, n % 2]
+            elif square_on_gpsimd(n):
+                sq = dz2_tiles[(n - 7) // 2][:].rearrange("p (n j) -> p n j", j=PACK)
             else:
                 sq_sb = work.tile([P, P, PACK], F32)
                 sq = sq_sb[:]
@@ -244,11 +243,11 @@ def tile_oddlayer_t_v_kernel(
 
         def times_g(q, lo=0, hi=2):
             if lo == 0:
-                dz2 = work.tile([P, 2 * P, PACK], BF16, align_bytes=64)
+                dz2 = work.tile([P, P * PACK], F32, align_bytes=64)
                 dz2_tiles[q] = dz2
             cols = slice(lo * P, hi * P)
             nc.vector.scalar_tensor_tensor(
-                out=dz2_tiles[q][:, cols, :], in0=m_tiles[q][:, lo:hi].rearrange("p h n j -> p (h n) j"), scalar=1.0,
+                out=dz2_tiles[q][:].bitcast(BF16).rearrange("p (m j) -> p m j", j=PACK)[:, cols, :], in0=m_tiles[q][:, lo:hi].rearrange("p h n j -> p (h n) j"), scalar=1.0,
                 in1=gT_tiles[q][:, :, cols].rearrange("p j m -> p m j"), op0=ALU.subtract, op1=ALU.mult,
             )
 
@@ -261,14 +260,14 @@ def tile_oddlayer_t_v_kernel(
             nc.vector.quantize_mx(
                 out=code_tiles[q][0][:, cols].bitcast(E5M2X4),
                 scales=code_tiles[q][1][:, cols],
-                in_=dz2_tiles[q][:, cols, :].rearrange("p m j -> p (m j)"),
+                in_=dz2_tiles[q][:].bitcast(BF16)[:, lo * P * PACK : hi * P * PACK],
             )
 
         def multiply(n):
             dz_codes, dz_scales = code_tiles[n // 2]
             cols = slice((n % 2) * P, (n % 2 + 1) * P)
             if n >= BLOCKS - 2:
-                out_ps = psum_a.tile([P, FEATURES], F32, tag="aT_ps")
+                out_ps = psum_a.tile([P, FEATURES], F32, tag="held_ps", bufs=3)
             else:
                 out_ps = psum_o.tile([P, FEATURES], F32)
             for again in range(1 + n % 2):
@@ -352,21 +351,23 @@ def tile_oddlayer_t_v_kernel(
         square(5)
         tanh(4)
         square(4)
+        transpose_a(7)
+        tanh(7)
         for q in range(1, PAIRS + 1):
             last = q == PAIRS - 1
             if q == 1:
-                quantise(0)
                 clip_of(3)
                 push_of(6)
                 quantise_weights()
                 absolute(4)
+                quantise(0)
                 times_g(1)
             elif q < PAIRS - 2:
                 clip_of(2 * q + 1)
                 push_of(2 * q + 4)
-                quantise(q - 1)
                 if is_pair(q + 3):
                     absolute(q + 3)
+                quantise(q - 1)
                 times_g(q)
             elif q == PAIRS - 2:
                 clip_of(2 * q + 1)
@@ -381,8 +382,9 @@ def tile_oddlayer_t_v_kernel(
                 quantise(q, 0, 1)
                 quantise(q, 1, 2)
             if is_pair(q + 2):
-                transpose_a(2 * q + 5)
                 transpose_a(2 * q + 4)
+            if is_pair(q + 3):
+                transpose_a(2 * q + 7)
             if q < PAIRS - 3:
                 multiply(2 * q - 2)
                 multiply(2 * q - 1)
@@ -393,14 +395,12 @@ def tile_oddlayer_t_v_kernel(
                 multiply(2 * q - 2)
                 multiply(2 * q - 1)
             if is_pair(q + 2):
-                tanh(2 * q + 5)
-                if square_on_gpsimd(2 * q + 5) and is_pair(q + 3):
-                    wait_for_vector(q + 3)
                 square(2 * q + 5)
+            if is_pair(q + 2):
                 tanh(2 * q + 4)
-                leave_psum(2 * q - 2)
+            leave_psum(2 * q - 2)
+            if is_pair(q + 2):
                 square(2 * q + 4)
-                leave_psum(2 * q - 1)
-            else:
-                leave_psum(2 * q - 2)
-                leave_psum(2 * q - 1)
+            if is_pair(q + 3):
+                tanh(2 * q + 7)
+            leave_psum(2 * q - 1)

@@ -138,7 +138,7 @@ def tile_oddlayer_t_v_kernel(
                 wmT_ps = psum_o.tile([P, 2, PACK, P], BF16, tag="out_ps")
                 wmT_tiles[r // 2] = wmT_ps
             for j in range(PACK):
-                turn_bf16(wmT_tiles[r // 2][:, r % 2, j, :], wm_sb[:, r, j * P : (j + 1) * P], True)
+                turn_bf16(wmT_tiles[r // 2][:, r % 2, j, :], wm_sb[:, r, j * P : (j + 1) * P], False)
 
         def group_weights(r):
             nc.scalar.copy(
@@ -163,7 +163,7 @@ def tile_oddlayer_t_v_kernel(
             )
 
         def mask_bf16(n):
-            return n % 4 == 2
+            return n % 8 != 0
 
         def push_of(n):
             if not pushed(n):
@@ -270,7 +270,7 @@ def tile_oddlayer_t_v_kernel(
                 out_ps = psum_a.tile([P, FEATURES], F32, tag="held_ps", bufs=3)
             else:
                 out_ps = psum_o.tile([P, FEATURES], F32)
-            for again in range(1 + n % 2):
+            for again in range(1 + (n % 2 == 1 and n < BLOCKS - 4)):
                 nc.tensor.matmul_mx(
                     out=out_ps[:],
                     lhsT=dz_codes[:, cols].bitcast(E5M2X4),

@@ -19,6 +19,7 @@ TOKENS = 4096
 FEATURES = 512
 CLIP = 10.0
 PUSH = 1024.0
+WB = {5: 3}
 BLOCKS = TOKENS // P
 PAIRS = BLOCKS // 2
 ROW_BLOCKS = FEATURES // P
@@ -88,10 +89,13 @@ def tile_oddlayer_t_v_kernel(
         warm = consts.tile([P, P], F32)
         nc.vector.memset(warm[:], 0.0)
 
-        def keep_warm(passes):
+        def keep_warm(passes, bank=None):
             for i in range(passes):
-                junk = psum_o.tile([P, P], F32, tag="out_ps")
-                nc.tensor.matmul(out=junk[:], lhsT=warm[:], rhs=warm[:], start=True, stop=True)
+                if bank is None:
+                    junk = psum_o.tile([P, P], F32, tag="out_ps")
+                    nc.tensor.matmul(out=junk[:], lhsT=warm[:], rhs=warm[:], start=True, stop=True)
+                else:
+                    nc.tensor.matmul(out=bank, lhsT=warm[:], rhs=warm[:], start=True, stop=True)
 
         wm_sb = consts.tile([P, ROW_BLOCKS, FEATURES], BF16)
         wm_grouped = consts.tile([P, FEATURES, PACK], BF16, align_bytes=64)
@@ -163,7 +167,7 @@ def tile_oddlayer_t_v_kernel(
             )
 
         def mask_bf16(n):
-            return n % 8 != 0
+            return n % 8 != 4
 
         def push_of(n):
             if not pushed(n):
@@ -174,9 +178,13 @@ def tile_oddlayer_t_v_kernel(
             )
             e_tiles[n] = e_sb
 
+        def warm_before(n):
+            return WB.get(n, 0)
+
         def transpose_a(n):
             held = n % 2 == 1 or n == 0
             aT_ps = psum_a.tile([P, PACK, P], F32, tag="held_ps" if held else "free_ps", bufs=3 if held else 1)
+            keep_warm(warm_before(n), aT_ps[:, 0, :])
             for j in range(PACK):
                 cols = slice(j * P, (j + 1) * P)
                 if pushed(n):
@@ -266,11 +274,11 @@ def tile_oddlayer_t_v_kernel(
         def multiply(n):
             dz_codes, dz_scales = code_tiles[n // 2]
             cols = slice((n % 2) * P, (n % 2 + 1) * P)
-            if n >= BLOCKS - 2:
+            if n >= BLOCKS - 3:
                 out_ps = psum_a.tile([P, FEATURES], F32, tag="held_ps", bufs=3)
             else:
                 out_ps = psum_o.tile([P, FEATURES], F32)
-            for again in range(1 + (n % 2 == 1 and n < BLOCKS - 4)):
+            for again in range(1):
                 nc.tensor.matmul_mx(
                     out=out_ps[:],
                     lhsT=dz_codes[:, cols].bitcast(E5M2X4),
@@ -372,8 +380,8 @@ def tile_oddlayer_t_v_kernel(
             elif q == PAIRS - 2:
                 clip_of(2 * q + 1)
                 times_g(q, 0, 1)
-                times_g(q, 1, 2)
                 quantise(q - 1)
+                times_g(q, 1, 2)
             elif last:
                 clip_of(2 * q + 1)
                 quantise(q - 1)

@@ -19,7 +19,7 @@ TOKENS = 4096
 FEATURES = 512
 CLIP = 10.0
 PUSH = 1024.0
-WB = {5: 3}
+WB = {5: 3, 7: 2}
 BLOCKS = TOKENS // P
 PAIRS = BLOCKS // 2
 ROW_BLOCKS = FEATURES // P
@@ -57,8 +57,10 @@ def tile_oddlayer_t_v_kernel(
         def load_z(q):
             z_sb = z_pool.tile([P, 2, FEATURES], F32)
             if q == 0:
-                for h in range(2):
-                    nc.sync.dma_start(out=z_sb[:, h, :], in_=z_view[q][:, h, :])
+                for c in range(2):
+                    cols = slice(c * (FEATURES // 2), (c + 1) * (FEATURES // 2))
+                    nc.sync.dma_start(out=z_sb[:, 0, cols], in_=z_view[q][:, 0, cols])
+                nc.sync.dma_start(out=z_sb[:, 1, :], in_=z_view[q][:, 1, :])
             else:
                 nc.sync.dma_start(out=z_sb[:], in_=z_view[q])
             z_tiles.append(z_sb)
@@ -145,10 +147,11 @@ def tile_oddlayer_t_v_kernel(
                 turn_bf16(wmT_tiles[r // 2][:, r % 2, j, :], wm_sb[:, r, j * P : (j + 1) * P], False)
 
         def group_weights(r):
-            nc.scalar.copy(
-                out=wm_grouped[:, r * P : (r + 1) * P, :],
-                in_=wmT_tiles[r // 2][:, r % 2].rearrange("p j i -> p i j"),
-            )
+            if r % 2 == 1:
+                nc.scalar.copy(
+                    out=wm_grouped[:, (r - 1) * P : (r + 1) * P, :].rearrange("p (r i) j -> p r i j", r=2),
+                    in_=wmT_tiles[r // 2][:].rearrange("p r j i -> p r i j"),
+                )
 
         def quantise_weights():
             nc.vector.quantize_mx(
@@ -278,16 +281,15 @@ def tile_oddlayer_t_v_kernel(
                 out_ps = psum_a.tile([P, FEATURES], F32, tag="held_ps", bufs=3)
             else:
                 out_ps = psum_o.tile([P, FEATURES], F32)
-            for again in range(1):
-                nc.tensor.matmul_mx(
-                    out=out_ps[:],
-                    lhsT=dz_codes[:, cols].bitcast(E5M2X4),
-                    lhsT_scale=dz_scales[:, cols],
-                    rhs=wm_codes[:].bitcast(E4M3X4),
-                    rhs_scale=wm_scales[:],
-                    start=True,
-                    stop=True,
-                )
+            nc.tensor.matmul_mx(
+                out=out_ps[:],
+                lhsT=dz_codes[:, cols].bitcast(E5M2X4),
+                lhsT_scale=dz_scales[:, cols],
+                rhs=wm_codes[:].bitcast(E4M3X4),
+                rhs_scale=wm_scales[:],
+                start=True,
+                stop=True,
+            )
             out_ps_tiles[n] = out_ps
 
         def leave_psum(n):
@@ -309,7 +311,7 @@ def tile_oddlayer_t_v_kernel(
                 nc.scalar.activation(
                     out=out_sb_tiles[n // 2][:, n % 2, :], in_=out_ps_tiles[n][:], func=ACT.Copy, scale=-0.5
                 )
-            if n >= BLOCKS - 6:
+            if n >= BLOCKS - 8:
                 nc.sync.dma_start(out=out_view[n // 2][:, n % 2, :], in_=out_sb_tiles[n // 2][:, n % 2, :])
             elif n % 2 == 1:
                 nc.sync.dma_start(out=out_view[n // 2], in_=out_sb_tiles[n // 2][:])
@@ -406,9 +408,9 @@ def tile_oddlayer_t_v_kernel(
                 square(2 * q + 5)
             if is_pair(q + 2):
                 tanh(2 * q + 4)
+            if is_pair(q + 3):
+                tanh(2 * q + 7)
             leave_psum(2 * q - 2)
             if is_pair(q + 2):
                 square(2 * q + 4)
-            if is_pair(q + 3):
-                tanh(2 * q + 7)
             leave_psum(2 * q - 1)

from contextlib import ExitStack

import concourse.mybir as mybir
from concourse.masks import make_identity

F32 = mybir.dt.float32
BF16 = mybir.dt.bfloat16
I32 = mybir.dt.int32
U32 = mybir.dt.uint32
U8 = mybir.dt.uint8
E4M3X4 = mybir.dt.float8_e4m3fn_x4
E5M2X4 = mybir.dt.float8_e5m2_x4
ALU = mybir.AluOpType
ACT = mybir.ActivationFunctionType

P = 128
PACK = 4
TOKENS = 4096
FEATURES = 512
CLIP = 10.0
PUSH = 1024.0
WB = {5: 3, 7: 2}
BLOCKS = TOKENS // P
PAIRS = BLOCKS // 2
ROW_BLOCKS = FEATURES // P

FLOPS = 2 * TOKENS * FEATURES * FEATURES
BYTES = TOKENS * FEATURES * (4 + 2 + 4) + 2 * FEATURES * FEATURES * 2


def tile_oddlayer_t_v_kernel(
    tc, x, llr, odd_weights, llr_weights, w_odd2even_mask, w_skipconn2even_mask, z, grad_out, out
):
    nc = tc.nc
    with ExitStack() as stack:
        stack.enter_context(tc.manual_schedule())
        consts = stack.enter_context(tc.tile_pool(name="consts", bufs=1))
        z_pool = stack.enter_context(tc.tile_pool(name="z_pool", bufs=PAIRS))
        g_pool = stack.enter_context(tc.tile_pool(name="g_pool", bufs=PAIRS))
        work = stack.enter_context(tc.tile_pool(name="work", bufs=5))
        out_pool = stack.enter_context(tc.tile_pool(name="out_pool", bufs=8))
        psum_a = stack.enter_context(tc.psum_pool(name="psum_a", bufs=4))
        psum_g = stack.enter_context(tc.psum_pool(name="psum_g", bufs=2))
        psum_o = stack.enter_context(tc.psum_pool(name="psum_o", bufs=2))

        z_view = z.rearrange("(q p h) k -> q p h k", p=P, h=2)
        g_view = grad_out.rearrange("(q p h) k -> q p h k", p=P, h=2)
        out_view = out.rearrange("(q p h) i -> q p h i", p=P, h=2)

        w_view = odd_weights.rearrange("(r p) k -> p r k", p=P)
        m_view = w_odd2even_mask.rearrange("(r p) k -> p r k", p=P)
        z_tiles = []
        g_tiles = []
        w_sb = consts.tile([P, ROW_BLOCKS, FEATURES], BF16)
        m_sb = consts.tile([P, ROW_BLOCKS, FEATURES], BF16)

        def load_z(q):
            z_sb = z_pool.tile([P, 2, FEATURES], F32)
            if q == 0:
                for c in range(2):
                    cols = slice(c * (FEATURES // 2), (c + 1) * (FEATURES // 2))
                    nc.sync.dma_start(out=z_sb[:, 0, cols], in_=z_view[q][:, 0, cols])
                nc.sync.dma_start(out=z_sb[:, 1, :], in_=z_view[q][:, 1, :])
            else:
                nc.sync.dma_start(out=z_sb[:], in_=z_view[q])
            z_tiles.append(z_sb)

        def load_g(q):
            g_sb = g_pool.tile([P, 2, FEATURES], BF16)
            nc.sync.dma_start(out=g_sb[:], in_=g_view[q])
            g_tiles.append(g_sb)

        load_z(0)
        load_z(1)
        for h in range(2):
            rows = slice(2 * h, 2 * h + 2)
            nc.sync.dma_start(out=w_sb[:, rows, :], in_=w_view[:, rows, :])
            nc.sync.dma_start(out=m_sb[:, rows, :], in_=m_view[:, rows, :])
            if h == 0:
                load_g(0)
        for q in range(2, PAIRS):
            load_z(q)
            load_g(q - 1)
        load_g(PAIRS - 1)

        ident_f32 = consts.tile([P, P], F32)
        make_identity(nc, ident_f32[:])
        ident_bf16 = consts.tile([P, P], BF16)
        make_identity(nc, ident_bf16[:])

        warm = consts.tile([P, P], F32)
        nc.vector.memset(warm[:], 0.0)

        def keep_warm(passes, bank=None):
            for i in range(passes):
                if bank is None:
                    junk = psum_o.tile([P, P], F32, tag="out_ps")
                    nc.tensor.matmul(out=junk[:], lhsT=warm[:], rhs=warm[:], start=True, stop=True)
                else:
                    nc.tensor.matmul(out=bank, lhsT=warm[:], rhs=warm[:], start=True, stop=True)

        wm_sb = consts.tile([P, ROW_BLOCKS, FEATURES], BF16)
        wm_grouped = consts.tile([P, FEATURES, PACK], BF16, align_bytes=64)
        wm_codes = consts.tile([P, FEATURES], U32, align_bytes=64)
        wm_scales = consts.tile([P, FEATURES], U8, align_bytes=64)
        wmT_tiles = {}
        a_tiles = {}
        e_tiles = {}
        aT_tiles = {}
        gT_tiles = {}
        th_tiles = {}
        sq_tiles = {}
        m_tiles = {}
        dz2_tiles = {}
        code_tiles = {}
        out_ps_tiles = {}
        out_sb_tiles = {}

        def is_block(n):
            return 0 <= n < BLOCKS

        def is_pair(q):
            return 0 <= q < PAIRS

        def pushed(n):
            q = n // 2
            return n % 2 == 0 and (2 <= q)

        def square_on_gpsimd(n):
            return n % 2 == 1 and 7 <= n < 32

        def turn_bf16(out_ps, in_sb, as_matmul):
            if as_matmul:
                nc.tensor.matmul(out=out_ps, lhsT=in_sb, rhs=ident_bf16[:], start=True, stop=True)
            else:
                nc.tensor.transpose(out_ps, in_sb, ident_bf16[:])

        def mask_weights(half):
            rows = slice(2 * half, 2 * half + 2)
            nc.vector.tensor_tensor(out=wm_sb[:, rows, :], in0=w_sb[:, rows, :], in1=m_sb[:, rows, :], op=ALU.mult)

        def transpose_weights(r):
            if r % 2 == 0:
                wmT_ps = psum_o.tile([P, 2, PACK, P], BF16, tag="out_ps")
                wmT_tiles[r // 2] = wmT_ps
            for j in range(PACK):
                turn_bf16(wmT_tiles[r // 2][:, r % 2, j, :], wm_sb[:, r, j * P : (j + 1) * P], False)

        def group_weights(r):
            if r % 2 == 1:
                nc.scalar.copy(
                    out=wm_grouped[:, (r - 1) * P : (r + 1) * P, :].rearrange("p (r i) j -> p r i j", r=2),
                    in_=wmT_tiles[r // 2][:].rearrange("p r j i -> p r i j"),
                )

        def quantise_weights():
            nc.vector.quantize_mx(
                out=wm_codes[:].bitcast(E4M3X4),
                scales=wm_scales[:],
                in_=wm_grouped[:].rearrange("p i j -> p (i j)"),
            )

        def absolute(q, lo=0, hi=2):
            if lo == 0:
                a_sb = work.tile([P, 2, FEATURES], F32)
                a_tiles[q] = a_sb
            nc.vector.tensor_single_scalar(
                out=a_tiles[q][:, lo:hi, :].bitcast(I32), in_=z_tiles[q][:, lo:hi, :].bitcast(I32),
                scalar=0x7FFFFFFF, op=ALU.bitwise_and,
            )

        def mask_bf16(n):
            return n % 8 != 4

        def push_of(n):
            if not pushed(n):
                return
            e_sb = work.tile([P, FEATURES], BF16 if mask_bf16(n) else F32, tag="e_bf" if mask_bf16(n) else "e_f32")
            nc.vector.tensor_scalar(
                out=e_sb[:], in0=a_tiles[n // 2][:, n % 2, :], scalar1=CLIP, scalar2=PUSH, op0=ALU.is_gt, op1=ALU.mult
            )
            e_tiles[n] = e_sb

        def warm_before(n):
            return WB.get(n, 0)

        def transpose_a(n):
            held = n % 2 == 1 or n == 0
            aT_ps = psum_a.tile([P, PACK, P], F32, tag="held_ps" if held else "free_ps", bufs=3 if held else 1)
            keep_warm(warm_before(n), aT_ps[:, 0, :])
            for j in range(PACK):
                cols = slice(j * P, (j + 1) * P)
                if pushed(n):
                    nc.tensor.matmul(
                        out=aT_ps[:, j, :], lhsT=a_tiles[n // 2][:, n % 2, cols], rhs=ident_f32[:],
                        is_transpose=True, start=True, stop=False,
                    )
                    if mask_bf16(n):
                        nc.tensor.matmul(out=aT_ps[:, j, :], lhsT=e_tiles[n][:, cols], rhs=ident_bf16[:], start=False, stop=True)
                    else:
                        nc.tensor.matmul(
                            out=aT_ps[:, j, :], lhsT=e_tiles[n][:, cols], rhs=ident_f32[:],
                            is_transpose=True, start=False, stop=True,
                        )
                else:
                    nc.tensor.transpose(aT_ps[:, j, :], a_tiles[n // 2][:, n % 2, cols], ident_f32[:])
            aT_tiles[n] = aT_ps

        def transpose_z0():
            zT_ps = psum_g.tile([P, PACK, P], F32, tag="gT_ps")
            for j in range(PACK):
                nc.tensor.transpose(zT_ps[:, j, :], z_tiles[0][:, 0, j * P : (j + 1) * P], ident_f32[:])
            aT_tiles["z0"] = zT_ps

        def transpose_g(n):
            q, h = n // 2, n % 2
            if h == 0:
                gT_ps = psum_g.tile([P, PACK, 2 * P], BF16)
                gT_tiles[q] = gT_ps
            for j in range(PACK):
                turn_bf16(gT_tiles[q][:, j, h * P : (h + 1) * P], g_tiles[q][:, h, j * P : (j + 1) * P], False)

        def tanh(n):
            th = work.tile([P, P, PACK], F32)
            nc.scalar.activation(
                out=th[:], in_=aT_tiles["z0" if n == 0 else n][:].rearrange("p j n -> p n j"), func=ACT.Tanh, scale=0.5
            )
            th_tiles[n] = th

        def square(n):
            if n // 2 not in m_tiles:
                m_sb = work.tile([P, 2, P, PACK], F32)
                m_tiles[n // 2] = m_sb
            if pushed(n):
                sq = m_tiles[n // 2][:, n % 2]
            elif square_on_gpsimd(n):
                sq = dz2_tiles[(n - 7) // 2][:].rearrange("p (n j) -> p n j", j=PACK)
            else:
                sq_sb = work.tile([P, P, PACK], F32)
                sq = sq_sb[:]
            if square_on_gpsimd(n):
                nc.gpsimd.tensor_tensor(out=sq, in0=th_tiles[n][:], in1=th_tiles[n][:], op=ALU.mult)
            else:
                nc.scalar.activation(out=sq, in_=th_tiles[n][:], func=ACT.Square)
            sq_tiles[n] = sq

        def clip_of(n):
            if pushed(n):
                return
            nc.vector.scalar_tensor_tensor(
                out=m_tiles[n // 2][:, n % 2], in0=aT_tiles[n][:].rearrange("p j n -> p n j"), scalar=CLIP,
                in1=sq_tiles[n], op0=ALU.is_gt, op1=ALU.max,
            )

        def times_g(q, lo=0, hi=2):
            if lo == 0:
                dz2 = work.tile([P, P * PACK], F32, align_bytes=64)
                dz2_tiles[q] = dz2
            cols = slice(lo * P, hi * P)
            nc.vector.scalar_tensor_tensor(
                out=dz2_tiles[q][:].bitcast(BF16).rearrange("p (m j) -> p m j", j=PACK)[:, cols, :], in0=m_tiles[q][:, lo:hi].rearrange("p h n j -> p (h n) j"), scalar=1.0,
                in1=gT_tiles[q][:, :, cols].rearrange("p j m -> p m j"), op0=ALU.subtract, op1=ALU.mult,
            )

        def quantise(q, lo=0, hi=2):
            if lo == 0:
                dz_codes = work.tile([P, 2 * P], U32, align_bytes=64)
                dz_scales = work.tile([P, 2 * P], U8, align_bytes=64)
                code_tiles[q] = (dz_codes, dz_scales)
            cols = slice(lo * P, hi * P)
            nc.vector.quantize_mx(
                out=code_tiles[q][0][:, cols].bitcast(E5M2X4),
                scales=code_tiles[q][1][:, cols],
                in_=dz2_tiles[q][:].bitcast(BF16)[:, lo * P * PACK : hi * P * PACK],
            )

        def multiply(n):
            dz_codes, dz_scales = code_tiles[n // 2]
            cols = slice((n % 2) * P, (n % 2 + 1) * P)
            if n >= BLOCKS - 3:
                out_ps = psum_a.tile([P, FEATURES], F32, tag="held_ps", bufs=3)
            else:
                out_ps = psum_o.tile([P, FEATURES], F32)
            nc.tensor.matmul_mx(
                out=out_ps[:],
                lhsT=dz_codes[:, cols].bitcast(E5M2X4),
                lhsT_scale=dz_scales[:, cols],
                rhs=wm_codes[:].bitcast(E4M3X4),
                rhs_scale=wm_scales[:],
                start=True,
                stop=True,
            )
            out_ps_tiles[n] = out_ps

        def leave_psum(n):
            if n % 2 == 0:
                out_sb = out_pool.tile([P, 2, FEATURES], F32)
                out_sb_tiles[n // 2] = out_sb
            if n == BLOCKS - 1:
                for cols in (slice(0, FEATURES // 2), slice(FEATURES // 2, FEATURES)):
                    nc.vector.tensor_scalar_mul(
                        out=out_sb_tiles[n // 2][:, 1, cols], in0=out_ps_tiles[n][:, cols], scalar1=-0.5
                    )
                    nc.sync.dma_start(out=out_view[n // 2][:, 1, cols], in_=out_sb_tiles[n // 2][:, 1, cols])
                return
            if n == BLOCKS - 3:
                nc.vector.tensor_scalar_mul(
                    out=out_sb_tiles[n // 2][:, n % 2, :], in0=out_ps_tiles[n][:], scalar1=-0.5
                )
            else:
                nc.scalar.activation(
                    out=out_sb_tiles[n // 2][:, n % 2, :], in_=out_ps_tiles[n][:], func=ACT.Copy, scale=-0.5
                )
            if n >= BLOCKS - 8:
                nc.sync.dma_start(out=out_view[n // 2][:, n % 2, :], in_=out_sb_tiles[n // 2][:, n % 2, :])
            elif n % 2 == 1:
                nc.sync.dma_start(out=out_view[n // 2], in_=out_sb_tiles[n // 2][:])

        keep_warm(3)
        transpose_z0()
        absolute(0, 0, 1)
        absolute(0, 1, 2)
        transpose_a(0)
        transpose_a(1)
        keep_warm(3)
        tanh(0)
        square(0)
        tanh(1)
        square(1)
        absolute(1)
        transpose_a(2)
        transpose_a(3)
        clip_of(0)
        mask_weights(0)
        transpose_g(0)
        transpose_g(1)
        tanh(2)
        square(2)
        transpose_weights(0)
        transpose_weights(1)
        clip_of(1)
        mask_weights(1)
        times_g(0)
        absolute(2)
        clip_of(2)
        push_of(4)
        absolute(3)
        tanh(3)
        group_weights(0)
        group_weights(1)
        square(3)
        transpose_weights(2)
        transpose_weights(3)
        transpose_a(5)
        transpose_a(4)
        transpose_g(2)
        transpose_g(3)
        group_weights(2)
        group_weights(3)
        tanh(5)
        square(5)
        tanh(4)
        square(4)
        transpose_a(7)
        tanh(7)
        for q in range(1, PAIRS + 1):
            last = q == PAIRS - 1
            if q == 1:
                clip_of(3)
                push_of(6)
                quantise_weights()
                absolute(4)
                quantise(0)
                times_g(1)
            elif q < PAIRS - 2:
                clip_of(2 * q + 1)
                push_of(2 * q + 4)
                if is_pair(q + 3):
                    absolute(q + 3)
                quantise(q - 1)
                times_g(q)
            elif q == PAIRS - 2:
                clip_of(2 * q + 1)
                times_g(q, 0, 1)
                quantise(q - 1)
                times_g(q, 1, 2)
            elif last:
                clip_of(2 * q + 1)
                quantise(q - 1)
                times_g(q, 0, 1)
                times_g(q, 1, 2)
                quantise(q, 0, 1)
                quantise(q, 1, 2)
            if is_pair(q + 2):
                transpose_a(2 * q + 4)
            if is_pair(q + 3):
                transpose_a(2 * q + 7)
            if q < PAIRS - 3:
                multiply(2 * q - 2)
                multiply(2 * q - 1)
            if is_pair(q + 1):
                transpose_g(2 * q + 2)
                transpose_g(2 * q + 3)
            if q >= PAIRS - 3:
                multiply(2 * q - 2)
                multiply(2 * q - 1)
            if is_pair(q + 2):
                square(2 * q + 5)
            if is_pair(q + 2):
                tanh(2 * q + 4)
            if is_pair(q + 3):
                tanh(2 * q + 7)
            leave_psum(2 * q - 2)
            if is_pair(q + 2):
                square(2 * q + 4)
            leave_psum(2 * q - 1)
